import numpy as np
import ml_dtypes


def mxq(x, axis, fmt="e4m3"):
    dtype, down = {"e4m3": (ml_dtypes.float8_e4m3fn, 7), "e5m2": (ml_dtypes.float8_e5m2, 14)}[fmt]
    v = np.moveaxis(np.asarray(x, np.float32).astype(ml_dtypes.bfloat16).astype(np.float64), axis, -1)
    blocks = v.reshape(v.shape[:-1] + (-1, 32))
    amax = np.abs(blocks).max(-1, keepdims=True)
    byte = np.maximum(np.where(amax > 0, np.frexp(amax)[1] - 1 + 127, 0) - down, 1)
    scale = np.exp2(byte - 127.0)
    codes = (blocks / scale).astype(np.float32).astype(dtype).astype(np.float64)
    return np.moveaxis((codes * scale).reshape(v.shape), -1, axis)


WIDE = False


def mx_kscale(k):
    if not WIDE:
        return np.ones(k)
    levels = np.array([10, -10, 5, -5, 0])
    a = np.random.permutation(np.resize(levels, k // 512 * 4)).reshape(k // 512, 4)
    idx = np.arange(k)
    return np.exp2(a[idx // 512, idx % 128 // 32])


BF16 = ml_dtypes.bfloat16


def bf(x):
    return np.asarray(x, np.float32).astype(BF16)


def f64(x):
    return np.asarray(x).astype(np.float64)


B, S, D, QR, KR, H, NOPE, ROPE, VD = 2, 256, 2048, 1536, 512, 16, 128, 64, 128
EPS = 1e-6
THETA = 10000.0
LAT = 3.0 * np.sqrt(EPS)


def rmsnorm(x, w):
    var = np.mean(x * x, axis=-1, keepdims=True)
    return w * (x * (1.0 / np.sqrt(var + EPS)))


def rope_cos_sin(seq_len):
    inv_freq = 1.0 / (THETA ** (f64(np.arange(0, ROPE, 2)) / ROPE))
    t = f64(np.arange(seq_len))
    freqs = np.outer(t, inv_freq)
    emb = np.concatenate([freqs, freqs], -1)
    return np.cos(emb), np.sin(emb)


def rotate_half(x):
    x1, x2 = x[..., : x.shape[-1] // 2], x[..., x.shape[-1] // 2 :]
    return np.concatenate([-x2, x1], axis=-1)


def setup_inputs():
    s, t = mx_kscale(D), mx_kscale(KR)
    return {"hidden_states": bf(np.random.standard_normal((B, S, D)) * s),
            "kv_a_w_ckv": bf(np.random.standard_normal((KR, D)) * LAT / np.sqrt(D) / s[None, :]),
            "k_pe_raw": bf(np.random.standard_normal((B, S, ROPE))),
            "kv_a_ln_w": bf((1.0 + 0.1 * np.random.standard_normal(KR)) * t),
            "kv_b_w": bf(np.random.standard_normal((H * (NOPE + VD), KR)) / np.sqrt(KR) / t[None, :])}


def reference(hidden_states, kv_a_w_ckv, k_pe_raw, kv_a_ln_w, kv_b_w):
    ckv = mxq(f64(hidden_states), 2, "e4m3") @ mxq(f64(kv_a_w_ckv), 1, "e4m3").T
    ckv_n = rmsnorm(ckv, f64(kv_a_ln_w))
    kv = mxq(ckv_n, 2, "e4m3") @ mxq(f64(kv_b_w), 1, "e4m3").T
    kv = kv.reshape(B, S, H, NOPE + VD).transpose(0, 2, 1, 3)
    k_nope, v = kv[..., :NOPE], kv[..., NOPE:]
    k_pe = f64(k_pe_raw).reshape(B, 1, S, ROPE)
    cos, sin = rope_cos_sin(S)
    cos, sin = cos[None, None], sin[None, None]
    k_pe = k_pe * cos + rotate_half(k_pe) * sin
    key_s = np.concatenate([k_nope, np.broadcast_to(k_pe, (B, H, S, ROPE))], -1)
    return key_s, v

@@ -1,0 +1,414 @@
+import math
+from contextlib import ExitStack
+
+import concourse.mybir as mybir
+from concourse.masks import make_identity
+
+F32 = mybir.dt.float32
+BF16 = mybir.dt.bfloat16
+I32 = mybir.dt.int32
+U32 = mybir.dt.uint32
+U8 = mybir.dt.uint8
+FP8X4 = mybir.dt.float8_e4m3fn_x4
+ALU = mybir.AluOpType
+ACT = mybir.ActivationFunctionType
+
+P = 128
+D_MODEL = 2048
+LATENT = 512
+HEADS = 16
+ROPE = 64
+EPS = 1e-6
+THETA = 10000.0
+FLOPS = 2 * 512 * D_MODEL * LATENT + 2 * 512 * LATENT * HEADS * 256
+
+
+ORDER = (
+    ("F", 0, "v"), ("T", "wa", 0, 0), ("F", 1, "v"), ("T", "wa", 0, 1), ("C", "wa", 0, 0, "s"),
+    ("F", 2, "v"), ("C", "wa", 0, 1, "v"), ("T", "wa", 1, 0), ("T", "wa", 1, 1), ("G",),
+    ("C", "wa", 1, 0, "s"), ("Q", "wa", 0), ("GC",), ("C", "wa", 1, 1, "s"), ("F", 3, "v"),
+    ("T", "wa", 2, 0), ("F", 4, "v"), ("T", "wa", 2, 1), ("C", "wa", 2, 0, "s"), ("Q", "wa", 1),
+    ("C", "wa", 2, 1, "s"), ("T", "wa", 3, 0), ("F", 5, "v"), ("T", "wa", 3, 1),
+    ("C", "wa", 3, 0, "s"), ("Q", "wa", 2), ("C", "wa", 3, 1, "s"), ("T", "x", 0, 0),
+    ("F", 6, "v"), ("T", "x", 0, 1), ("C", "x", 0, 0, "s"), ("Q", "wa", 3), ("C", "x", 0, 1, "s"),
+    ("F", 7, "v"), ("T", "x", 1, 0), ("T", "x", 1, 1), ("C", "x", 1, 0, "s"), ("Q", "x", 0),
+    ("C", "x", 1, 1, "s"), ("T", "x", 2, 0), ("T", "x", 2, 1), ("C", "x", 2, 0, "s"),
+    ("Q", "x", 1), ("M1", 0), ("C", "x", 2, 1, "s"), ("Q", "x", 2), ("T", "x", 3, 0), ("SQ", 0),
+    ("T", "x", 3, 1), ("C", "x", 3, 0, "v"), ("M1", 1), ("C", "x", 3, 1, "s"), ("NV", 0),
+    ("Q", "x", 3), ("CT", 0), ("SQ", 1), ("T", "wb", 0, 0), ("CC", 0, "v"), ("T", "wb", 0, 1),
+    ("CQ", 0), ("M1", 2), ("CW", 0, "s"), ("NV", 1), ("CT", 1), ("Q", "wb", 0), ("SQ", 2),
+    ("T", "wb", 1, 0), ("CC", 1, "v"), ("T", "wb", 1, 1), ("M2", 0, 0), ("CW", 1, "s"), ("CQ", 1),
+    ("NV", 2), ("M1", 3), ("D", 0, 0, "v"), ("M2", 0, 1), ("SQ", 3), ("Q", "wb", 1), ("CT", 2),
+    ("T", "wb", 2, 0), ("D", 0, 1, "v"), ("CC", 2, "s"), ("M2", 1, 0), ("NV", 3), ("ST", 0, "A"),
+    ("M2", 1, 1), ("D", 1, 0, "s"), ("T", "wb", 2, 1), ("CQ", 2), ("D", 1, 1, "s"), ("CT", 3),
+    ("CW", 2, "v"), ("T", "wb", 3, 0), ("CC", 3, "s"), ("M2", 0, 2), ("ST", 1, "A"), ("M2", 1, 2),
+    ("D", 0, 2, "s"), ("CQ", 3), ("T", "wb", 3, 1), ("Q", "wb", 2), ("D", 1, 2, "s"), ("M2", 0, 3),
+    ("CW", 3, "v"), ("M2", 1, 3), ("D", 0, 3, "s"), ("M2", 2, 0), ("M2", 2, 1), ("D", 2, 0, "s"),
+    ("ST", 0, "B"), ("M2", 2, 2), ("D", 2, 1, "v"), ("M2", 2, 3), ("D", 2, 2, "s"),
+    ("T", "wb", 4, 0), ("D", 2, 3, "v"), ("T", "wb", 4, 1), ("D", 1, 3, "s"), ("Q", "wb", 3),
+    ("T", "wb", 5, 0), ("ST", 2, "W"), ("T", "wb", 5, 1), ("CW", 4, "s"), ("T", "wb", 6, 0),
+    ("CW", 5, "v"), ("M2", 3, 0), ("ST", 1, "B"), ("M2", 3, 1), ("D", 3, 0, "s"), ("M2", 3, 2),
+    ("D", 3, 1, "v"), ("M2", 3, 3), ("D", 3, 2, "s"), ("T", "wb", 6, 1), ("D", 3, 3, "v"),
+    ("T", "wb", 7, 0), ("CW", 6, "s"), ("T", "wb", 7, 1), ("Q", "wb", 4), ("ST", 3, "W"),
+    ("Q", "wb", 5), ("CW", 7, "s"), ("M2", 4, 0), ("Q", "wb", 6), ("M2", 4, 1), ("M2", 4, 2),
+    ("D", 4, 0, "v"), ("M2", 4, 3), ("D", 4, 1, "s"), ("M2", 5, 0), ("D", 4, 2, "v"), ("M2", 5, 1),
+    ("D", 4, 3, "s"), ("M2", 5, 2), ("D", 5, 0, "v"), ("M2", 5, 3), ("D", 5, 1, "s"),
+    ("ST", 4, "W"), ("M2", 6, 0), ("M2", 6, 1), ("D", 5, 2, "v"), ("D", 5, 3, "s"), ("M2", 6, 2),
+    ("M2", 6, 3), ("D", 6, 0, "v"), ("D", 6, 1, "s"), ("ST", 5, "W"), ("D", 6, 2, "v"),
+    ("D", 6, 3, "s"), ("Q", "wb", 7), ("M2", 7, 0), ("M2", 7, 1), ("D", 7, 0, "s"), ("M2", 7, 2),
+    ("D", 7, 1, "v"), ("M2", 7, 3), ("D", 7, 2, "s"), ("D", 7, 3, "v"), ("ST", 6, "W"),
+    ("ST", 7, "W"),
+)
+
+
+def tile_modelnew_pb_kernel(
+    tc, hidden_states, kv_a_w_ckv, k_pe_raw, kv_a_ln_w, kv_b_w, out_0, out_1
+):
+    nc = tc.nc
+    with ExitStack() as ctx:
+        ctx.enter_context(tc.manual_schedule())
+        const = ctx.enter_context(tc.tile_pool(name="const", bufs=1))
+        raw = ctx.enter_context(tc.tile_pool(name="raw", bufs=1))
+        keep = ctx.enter_context(tc.tile_pool(name="keep", bufs=1))
+        outs = ctx.enter_context(tc.tile_pool(name="outs", bufs=1))
+        grp = ctx.enter_context(tc.tile_pool(name="grp", bufs=4))
+        work = ctx.enter_context(tc.tile_pool(name="work", bufs=4))
+        psum = ctx.enter_context(tc.psum_pool(name="psum", bufs=8))
+
+        kpe = const.tile([P, 4, ROPE], BF16)
+        for b in range(2):
+            nc.scalar.dma_start(
+                out=kpe[b:P:2, :, :],
+                in_=k_pe_raw[b].rearrange("(q j) d -> q j d", j=4),
+            )
+        gain_row = const.tile([P, LATENT], BF16)
+        nc.vector.memset(gain_row[:], 0.0)
+        nc.scalar.dma_start(
+            out=gain_row[0:1, :], in_=kv_a_ln_w.rearrange("(o n) -> o n", o=1)
+        )
+
+        raws = {}
+        wa_view = kv_a_w_ckv.rearrange("(u p e) k -> u e p k", u=2, e=2)
+        for t in range(4):
+            wa_r = raw.tile([P, D_MODEL], BF16, name="wa_raw%d" % t)
+            nc.sync.dma_start(out=wa_r[:], in_=wa_view[t // 2, t % 2])
+            raws[("wa", t)] = wa_r
+        x_view = hidden_states.rearrange("b (q j) k -> b j q k", j=4)
+        for j in range(4):
+            x_r = raw.tile([P, D_MODEL], BF16, name="x_raw%d" % j)
+            for b in range(2):
+                nc.sync.dma_start(out=x_r[b:P:2, :], in_=x_view[b, j])
+            raws[("x", j)] = x_r
+        wb_view = kv_b_w.rearrange("(c p j) k -> c p (j k)", c=8, j=4)
+        for c in range(8):
+            wb_r = raw.tile([P, 4 * LATENT], BF16, name="wb_raw%d" % c)
+            nc.sync.dma_start(out=wb_r[:], in_=wb_view[c])
+            raws[("wb", c)] = wb_r
+
+        twice_p = const.tile([P, 4], I32)
+        nc.gpsimd.iota(out=twice_p[:], pattern=[[0, 4]], base=0, channel_multiplier=2)
+        j_idx = const.tile([P, 4], I32)
+        nc.gpsimd.iota(out=j_idx[:], pattern=[[1, 4]], base=0, channel_multiplier=0)
+        ident_f = const.tile([P, P], F32)
+        make_identity(nc, ident_f[:])
+        ident_b = const.tile([P, P], BF16)
+        make_identity(nc, ident_b[:])
+        ones_b = const.tile([P, P], BF16)
+        nc.vector.memset(ones_b[:], 1.0)
+        eps_t = const.tile([P, 1], F32)
+        nc.vector.memset(eps_t[:], EPS)
+        zero_t = const.tile([P, 1], F32)
+        nc.vector.memset(zero_t[:], 0.0)
+
+        warm_sin = const.tile([P, 1], F32)
+        nc.scalar.activation(out=warm_sin[:], in_=zero_t[:], func=ACT.Sin)
+
+        four_q = const.tile([P, 4], I32)
+        nc.vector.tensor_single_scalar(
+            out=four_q[:], in_=twice_p[:], scalar=0x1FC, op=ALU.bitwise_and
+        )
+        pos = const.tile([P, 4], F32)
+        nc.vector.tensor_tensor(out=pos[:], in0=four_q[:], in1=j_idx[:], op=ALU.add)
+        turns = const.tile([P, 2, 4, 32], F32)
+        nc.vector.tensor_scalar(
+            out=turns[:, 0, :, 0:1],
+            in0=pos[:].unsqueeze(2),
+            scalar1=1.0 / (2.0 * math.pi),
+            scalar2=None,
+            op0=ALU.mult,
+        )
+        ratio = THETA ** (-1.0 / 32.0)
+        for w in (1, 2, 4, 8, 16):
+            nc.vector.tensor_scalar(
+                out=turns[:, 0, :, w : 2 * w],
+                in0=turns[:, 0, :, 0:w],
+                scalar1=ratio**w,
+                scalar2=None,
+                op0=ALU.mult,
+            )
+        nc.vector.tensor_scalar(
+            out=turns[:, 1], in0=turns[:, 0], scalar1=0.25, scalar2=None, op0=ALU.add
+        )
+        turns_flat = turns[:].rearrange("p c j f -> p (c j f)")
+        whole_i = const.tile([P, 256], I32)
+        nc.vector.tensor_copy(out=whole_i[:], in_=turns_flat)
+        whole_f = const.tile([P, 256], F32)
+        nc.vector.tensor_copy(out=whole_f[:], in_=whole_i[:])
+        frac = const.tile([P, 256], F32)
+        nc.vector.tensor_tensor(
+            out=frac[:], in0=turns_flat, in1=whole_f[:], op=ALU.subtract
+        )
+        neg_frac = const.tile([P, 256], F32)
+        nc.vector.scalar_tensor_tensor(
+            out=neg_frac[:],
+            in0=frac[:],
+            scalar=0.5,
+            in1=frac[:],
+            op0=ALU.is_gt,
+            op1=ALU.subtract,
+        )
+        sincos = const.tile([P, 2, 4, 32], F32)
+        nc.scalar.activation(
+            out=sincos[:].rearrange("p c j f -> p (c j f)"),
+            in_=neg_frac[:],
+            func=ACT.Sin,
+            scale=-2.0 * math.pi,
+        )
+        warm_sqrt = const.tile([P, 1], F32)
+        nc.scalar.activation(out=warm_sqrt[:], in_=eps_t[:], func=ACT.Sqrt)
+
+        sin_t = sincos[:, 0]
+        cos_t = sincos[:, 1]
+        rope_a = const.tile([P, 4, ROPE], F32)
+        nc.vector.tensor_tensor(
+            out=rope_a[:].rearrange("p j (h f) -> p j h f", h=2),
+            in0=kpe[:].rearrange("p j (h f) -> p j h f", h=2),
+            in1=cos_t.unsqueeze(2).to_broadcast([P, 4, 2, 32]),
+            op=ALU.mult,
+        )
+        rope_b = const.tile([P, 4, ROPE], F32)
+        nc.vector.scalar_tensor_tensor(
+            out=rope_b[:, :, 0:32],
+            in0=kpe[:, :, 32:64],
+            scalar=-1.0,
+            in1=sin_t,
+            op0=ALU.mult,
+            op1=ALU.mult,
+        )
+        nc.vector.tensor_tensor(
+            out=rope_b[:, :, 32:64], in0=kpe[:, :, 0:32], in1=sin_t, op=ALU.mult
+        )
+        rope = const.tile([P, 4, ROPE], F32)
+        nc.vector.tensor_tensor(out=rope[:], in0=rope_a[:], in1=rope_b[:], op=ALU.add)
+
+        gain_bc = const.tile([P, LATENT], F32)
+
+        wa_codes = keep.tile([P, 4, LATENT], U32, align_bytes=64)
+        wa_scales = keep.tile([P, 4, LATENT], U8, align_bytes=64)
+        x_codes = keep.tile([P, 4, 4, P], U32, align_bytes=64)
+        x_scales = keep.tile([P, 4, 4, P], U8, align_bytes=64)
+        c_codes = keep.tile([P, 4, P], U32, align_bytes=64)
+        c_scales = keep.tile([P, 4, P], U8, align_bytes=64)
+        wb_codes = keep.tile([P, 8, 512], U32, align_bytes=64)
+        wb_scales = keep.tile([P, 8, 512], U8, align_bytes=64)
+
+        key_view = out_0.rearrange("b h (q j) d -> b q h j d", j=4)
+        val_view = out_1.rearrange("b h (q j) d -> b q h j d", j=4)
+
+        live = {}
+
+        def copy_on(engine, out, in_):
+            if engine == "v":
+                nc.vector.tensor_copy(out=out, in_=in_)
+            else:
+                nc.scalar.copy(out=out, in_=in_)
+
+        def grouped_tile(kind, idx):
+            if ("g", kind, idx) not in live:
+                grouped = grp.tile([P, 4 * 512], BF16, tag="grouped", align_bytes=64)
+                live[("g", kind, idx)] = grouped
+            return live[("g", kind, idx)]
+
+        def out_tiles(c):
+            if ("key", c) not in live:
+                key_t = outs.tile([P, 2, 4, 192], F32, name="key%d" % c)
+                val_t = outs.tile([P, 2, 4, P], F32, name="val%d" % c)
+                live[("key", c)] = key_t
+                live[("val", c)] = val_t
+            return live[("key", c)], live[("val", c)]
+
+        for step in ORDER:
+            op = step[0]
+            if op == "G":
+                gain_ps = psum.tile([P, LATENT], F32, tag="bank")
+                nc.tensor.matmul(
+                    out=gain_ps[:], lhsT=ones_b[:], rhs=gain_row[:], start=True, stop=True
+                )
+                live["gain_ps"] = gain_ps
+            elif op == "GC":
+                nc.vector.tensor_copy(
+                    out=gain_bc[:].rearrange("q (u e p) -> q u e p", u=2, e=2),
+                    in_=live["gain_ps"][:].rearrange("q (u p e) -> q u e p", u=2, e=2),
+                )
+            elif op == "T":
+                kind, idx, h = step[1], step[2], step[3]
+                words = raws[(kind, idx)][:].bitcast(F32)
+                bank = psum.tile([P, 512], F32, tag="bank")
+                for m in range(4):
+                    col = (4 * h + m) * P
+                    nc.tensor.transpose(
+                        out=bank[:, m * P : (m + 1) * P],
+                        in_=words[:, col : col + P],
+                        identity=ident_f[:],
+                    )
+                live[("t", kind, idx, h)] = bank
+            elif op == "C":
+                kind, idx, h, engine = step[1], step[2], step[3], step[4]
+                view = (
+                    grouped_tile(kind, idx)[:]
+                    .bitcast(F32)
+                    .rearrange("q (g c u) -> q g c u", g=4, u=2)
+                )
+                copy_on(
+                    engine,
+                    view[:, 2 * h : 2 * h + 2],
+                    live[("t", kind, idx, h)][:].rearrange("q (g u c) -> q g c u", g=2, u=2),
+                )
+            elif op == "CW":
+                idx, engine = step[1], step[2]
+                view = (
+                    grouped_tile("wb", idx)[:]
+                    .bitcast(F32)
+                    .rearrange("q (p a m) -> q a p m", a=2, m=4)
+                )
+                for a in range(2):
+                    copy_on(
+                        engine,
+                        view[:, a],
+                        live[("t", "wb", idx, a)][:].rearrange("q (m p) -> q p m", m=4),
+                    )
+            elif op == "Q":
+                kind, idx = step[1], step[2]
+                grouped = live[("g", kind, idx)]
+                if kind == "wa":
+                    for g in range(4):
+                        nc.vector.quantize_mx(
+                            out=wa_codes[:, g, idx * P : (idx + 1) * P].bitcast(FP8X4),
+                            scales=wa_scales[:, g, idx * P : (idx + 1) * P],
+                            in_=grouped[:, g * 512 : (g + 1) * 512],
+                        )
+                elif kind == "x":
+                    nc.vector.quantize_mx(
+                        out=x_codes[:, idx].rearrange("q g c -> q (g c)").bitcast(FP8X4),
+                        scales=x_scales[:, idx].rearrange("q g c -> q (g c)"),
+                        in_=grouped[:],
+                    )
+                else:
+                    nc.vector.quantize_mx(
+                        out=wb_codes[:, idx, :].bitcast(FP8X4),
+                        scales=wb_scales[:, idx, :],
+                        in_=grouped[:],
+                    )
+            elif op == "M1":
+                j = step[1]
+                acc = psum.tile([P, LATENT], F32, tag="bank")
+                for g in range(4):
+                    nc.tensor.matmul_mx(
+                        out=acc[:],
+                        lhsT=x_codes[:, j, g, :].bitcast(FP8X4),
+                        lhsT_scale=x_scales[:, j, g, :],
+                        rhs=wa_codes[:, g, :].bitcast(FP8X4),
+                        rhs_scale=wa_scales[:, g, :],
+                        start=(g == 0),
+                        stop=(g == 3),
+                    )
+                live[("acc", j)] = acc
+            elif op == "SQ":
+                j = step[1]
+                squares = work.tile([P, LATENT], BF16, tag="squares")
+                ssq = work.tile([P, 1], F32, tag="ssq")
+                nc.scalar.activation(
+                    out=squares[:], in_=live[("acc", j)][:], func=ACT.Square, accum_out=ssq[:]
+                )
+                std = work.tile([P, 1], F32, tag="std")
+                nc.scalar.activation(
+                    out=std[:], in_=ssq[:], func=ACT.Sqrt, bias=eps_t[:], scale=1.0 / LATENT
+                )
+                live[("std", j)] = std
+            elif op == "NV":
+                j = step[1]
+                rstd = work.tile([P, 1], F32, tag="rstd")
+                nc.vector.reciprocal(out=rstd[:], in_=live[("std", j)][:])
+                normed = work.tile([P, LATENT], BF16, tag="normed")
+                nc.vector.scalar_tensor_tensor(
+                    out=normed[:],
+                    in0=live[("acc", j)][:],
+                    scalar=rstd[:],
+                    in1=gain_bc[:],
+                    op0=ALU.mult,
+                    op1=ALU.mult,
+                )
+                live[("normed", j)] = normed
+            elif op == "CT":
+                j = step[1]
+                bank = psum.tile([P, 4, P], BF16, tag="bank")
+                for t in range(4):
+                    nc.tensor.transpose(
+                        out=bank[:, t, :],
+                        in_=live[("normed", j)][:, t * P : (t + 1) * P],
+                        identity=ident_b[:],
+                    )
+                live[("ct", j)] = bank
+            elif op == "CC":
+                j, engine = step[1], step[2]
+                cgrouped = work.tile([P, P, 4], BF16, tag="cgrouped", align_bytes=64)
+                copy_on(engine, cgrouped[:], live[("ct", j)][:].rearrange("q t c -> q c t"))
+                live[("cg", j)] = cgrouped
+            elif op == "CQ":
+                j = step[1]
+                nc.vector.quantize_mx(
+                    out=c_codes[:, j, :].bitcast(FP8X4),
+                    scales=c_scales[:, j, :],
+                    in_=live[("cg", j)][:].rearrange("q c t -> q (c t)"),
+                )
+            elif op == "F":
+                c, engine = step[1], step[2]
+                key_t, val_t = out_tiles(c)
+                copy_on(
+                    engine,
+                    key_t[:, :, :, P:192],
+                    rope[:].unsqueeze(1).to_broadcast([P, 2, 4, ROPE]),
+                )
+            elif op == "M2":
+                c, j = step[1], step[2]
+                acc = psum.tile([P, 512], F32, tag="bank")
+                nc.tensor.matmul_mx(
+                    out=acc[:],
+                    lhsT=c_codes[:, j, :].bitcast(FP8X4),
+                    lhsT_scale=c_scales[:, j, :],
+                    rhs=wb_codes[:, c, :].bitcast(FP8X4),
+                    rhs_scale=wb_scales[:, c, :],
+                    start=True,
+                    stop=True,
+                )
+                live[("o", c, j)] = acc
+            elif op == "D":
+                c, j, engine = step[1], step[2], step[3]
+                key_t, val_t = out_tiles(c)
+                parts = live[("o", c, j)][:].rearrange("p (h s d) -> p h s d", h=2, s=2)
+                copy_on(engine, key_t[:, :, j, 0:P], parts[:, :, 0, :])
+                copy_on(engine, val_t[:, :, j, :], parts[:, :, 1, :])
+            else:
+                assert op == "ST"
+                c, part = step[1], step[2]
+                key_t, val_t = out_tiles(c)
+                j0, j1 = {"A": (0, 2), "B": (2, 4), "W": (0, 4)}[part]
+                for b in range(2):
+                    nc.sync.dma_start(
+                        out=key_view[b, :, 2 * c : 2 * c + 2, j0:j1, :],
+                        in_=key_t[b:P:2, :, j0:j1, :],
+                    )
+                    nc.sync.dma_start(
+                        out=val_view[b, :, 2 * c : 2 * c + 2, j0:j1, :],
+                        in_=val_t[b:P:2, :, j0:j1, :],
+                    )

@@ -24,21 +24,22 @@ FLOPS = 2 * 512 * D_MODEL * LATENT + 2 * 512 * LATENT * HEADS * 256
 
 
 ORDER = (
-    ("F", 0, "v"), ("T", "wa", 0, 0), ("F", 1, "v"), ("T", "wa", 0, 1), ("C", "wa", 0, 0, "s"),
-    ("F", 2, "v"), ("C", "wa", 0, 1, "v"), ("T", "wa", 1, 0), ("T", "wa", 1, 1), ("G",),
-    ("C", "wa", 1, 0, "s"), ("Q", "wa", 0), ("GC",), ("C", "wa", 1, 1, "s"), ("F", 3, "v"),
-    ("T", "wa", 2, 0), ("F", 4, "v"), ("T", "wa", 2, 1), ("C", "wa", 2, 0, "s"), ("Q", "wa", 1),
-    ("C", "wa", 2, 1, "s"), ("T", "wa", 3, 0), ("F", 5, "v"), ("T", "wa", 3, 1),
-    ("C", "wa", 3, 0, "s"), ("Q", "wa", 2), ("C", "wa", 3, 1, "s"), ("T", "x", 0, 0),
-    ("F", 6, "v"), ("T", "x", 0, 1), ("C", "x", 0, 0, "s"), ("Q", "wa", 3), ("C", "x", 0, 1, "s"),
-    ("F", 7, "v"), ("T", "x", 1, 0), ("T", "x", 1, 1), ("C", "x", 1, 0, "s"), ("Q", "x", 0),
-    ("C", "x", 1, 1, "s"), ("T", "x", 2, 0), ("T", "x", 2, 1), ("C", "x", 2, 0, "s"),
-    ("Q", "x", 1), ("M1", 0), ("C", "x", 2, 1, "s"), ("Q", "x", 2), ("T", "x", 3, 0), ("SQ", 0),
-    ("T", "x", 3, 1), ("C", "x", 3, 0, "v"), ("M1", 1), ("C", "x", 3, 1, "s"), ("NV", 0),
-    ("Q", "x", 3), ("CT", 0), ("SQ", 1), ("T", "wb", 0, 0), ("CC", 0, "v"), ("T", "wb", 0, 1),
-    ("CQ", 0), ("M1", 2), ("CW", 0, "s"), ("NV", 1), ("CT", 1), ("Q", "wb", 0), ("SQ", 2),
-    ("T", "wb", 1, 0), ("CC", 1, "v"), ("T", "wb", 1, 1), ("M2", 0, 0), ("CW", 1, "s"), ("CQ", 1),
-    ("NV", 2), ("M1", 3), ("D", 0, 0, "v"), ("M2", 0, 1), ("SQ", 3), ("Q", "wb", 1), ("CT", 2),
+    ("W", 9), ("F", 0, "v"), ("T", "wa", 0, 0), ("F", 1, "v"), ("T", "wa", 0, 1), ("W", 1),
+    ("C", "wa", 0, 0, "s"), ("F", 2, "v"), ("C", "wa", 0, 1, "v"), ("T", "wa", 1, 0),
+    ("T", "wa", 1, 1), ("W", 1), ("G",), ("C", "wa", 1, 0, "s"), ("Q", "wa", 0), ("GC",),
+    ("C", "wa", 1, 1, "s"), ("F", 3, "v"), ("T", "wa", 2, 0), ("F", 4, "v"), ("T", "wa", 2, 1),
+    ("W", 1), ("C", "wa", 2, 0, "s"), ("Q", "wa", 1), ("C", "wa", 2, 1, "s"), ("T", "wa", 3, 0),
+    ("F", 5, "v"), ("T", "wa", 3, 1), ("W", 1), ("C", "wa", 3, 0, "s"), ("Q", "wa", 2),
+    ("C", "wa", 3, 1, "s"), ("T", "x", 0, 0), ("F", 6, "v"), ("T", "x", 0, 1), ("W", 1),
+    ("C", "x", 0, 0, "s"), ("Q", "wa", 3), ("C", "x", 0, 1, "s"), ("F", 7, "v"), ("T", "x", 1, 0),
+    ("T", "x", 1, 1), ("W", 1), ("C", "x", 1, 0, "s"), ("Q", "x", 0), ("C", "x", 1, 1, "s"),
+    ("T", "x", 2, 0), ("T", "x", 2, 1), ("W", 1), ("C", "x", 2, 0, "s"), ("Q", "x", 1), ("M1", 0),
+    ("C", "x", 2, 1, "s"), ("Q", "x", 2), ("T", "x", 3, 0), ("SQ", 0), ("T", "x", 3, 1), ("W", 1),
+    ("C", "x", 3, 0, "v"), ("M1", 1), ("C", "x", 3, 1, "s"), ("NV", 0), ("Q", "x", 3), ("CT", 0),
+    ("SQ", 1), ("T", "wb", 0, 0), ("CC", 0, "v"), ("T", "wb", 0, 1), ("CQ", 0), ("M1", 2),
+    ("CW", 0, "s"), ("NV", 1), ("CT", 1), ("Q", "wb", 0), ("SQ", 2), ("T", "wb", 1, 0),
+    ("CC", 1, "v"), ("T", "wb", 1, 1), ("M2", 0, 0), ("CW", 1, "s"), ("CQ", 1), ("NV", 2),
+    ("M1", 3), ("D", 0, 0, "v"), ("M2", 0, 1), ("SQ", 3), ("Q", "wb", 1), ("CT", 2),
     ("T", "wb", 2, 0), ("D", 0, 1, "v"), ("CC", 2, "s"), ("M2", 1, 0), ("NV", 3), ("ST", 0, "A"),
     ("M2", 1, 1), ("D", 1, 0, "s"), ("T", "wb", 2, 1), ("CQ", 2), ("D", 1, 1, "s"), ("CT", 3),
     ("CW", 2, "v"), ("T", "wb", 3, 0), ("CC", 3, "s"), ("M2", 0, 2), ("ST", 1, "A"), ("M2", 1, 2),
@@ -81,6 +82,10 @@ def tile_modelnew_pb_kernel(
                 out=kpe[b:P:2, :, :],
                 in_=k_pe_raw[b].rearrange("(q j) d -> q j d", j=4),
             )
+        ones_b = const.tile([P, P], BF16)
+        nc.vector.memset(ones_b[:], 1.0)
+        warm_rhs = const.tile([P, 512], BF16)
+        nc.vector.memset(warm_rhs[:], 0.0)
         gain_row = const.tile([P, LATENT], BF16)
         nc.vector.memset(gain_row[:], 0.0)
         nc.scalar.dma_start(
@@ -113,8 +118,6 @@ def tile_modelnew_pb_kernel(
         make_identity(nc, ident_f[:])
         ident_b = const.tile([P, P], BF16)
         make_identity(nc, ident_b[:])
-        ones_b = const.tile([P, P], BF16)
-        nc.vector.memset(ones_b[:], 1.0)
         eps_t = const.tile([P, 1], F32)
         nc.vector.memset(eps_t[:], EPS)
         zero_t = const.tile([P, 1], F32)
@@ -239,7 +242,15 @@ def tile_modelnew_pb_kernel(
 
         for step in ORDER:
             op = step[0]
-            if op == "G":
+            if op == "W":
+                if "warm" not in live:
+                    warm_ps = psum.tile([P, 512], F32, tag="bank")
+                    live["warm"] = warm_ps
+                for rep in range(step[1]):
+                    nc.tensor.matmul(
+                        out=live["warm"][:], lhsT=ones_b[:], rhs=warm_rhs[:], start=True, stop=True
+                    )
+            elif op == "G":
                 gain_ps = psum.tile([P, LATENT], F32, tag="bank")
                 nc.tensor.matmul(
                     out=gain_ps[:], lhsT=ones_b[:], rhs=gain_row[:], start=True, stop=True

@@ -24,40 +24,40 @@ FLOPS = 2 * 512 * D_MODEL * LATENT + 2 * 512 * LATENT * HEADS * 256
 
 
 ORDER = (
-    ("W", 9), ("F", 0, "v"), ("T", "wa", 0, 0), ("F", 1, "v"), ("T", "wa", 0, 1), ("W", 1),
-    ("C", "wa", 0, 0, "s"), ("F", 2, "v"), ("C", "wa", 0, 1, "v"), ("T", "wa", 1, 0),
-    ("T", "wa", 1, 1), ("W", 1), ("G",), ("C", "wa", 1, 0, "s"), ("Q", "wa", 0), ("GC",),
-    ("C", "wa", 1, 1, "s"), ("F", 3, "v"), ("T", "wa", 2, 0), ("F", 4, "v"), ("T", "wa", 2, 1),
-    ("W", 1), ("C", "wa", 2, 0, "s"), ("Q", "wa", 1), ("C", "wa", 2, 1, "s"), ("T", "wa", 3, 0),
-    ("F", 5, "v"), ("T", "wa", 3, 1), ("W", 1), ("C", "wa", 3, 0, "s"), ("Q", "wa", 2),
-    ("C", "wa", 3, 1, "s"), ("T", "x", 0, 0), ("F", 6, "v"), ("T", "x", 0, 1), ("W", 1),
-    ("C", "x", 0, 0, "s"), ("Q", "wa", 3), ("C", "x", 0, 1, "s"), ("F", 7, "v"), ("T", "x", 1, 0),
-    ("T", "x", 1, 1), ("W", 1), ("C", "x", 1, 0, "s"), ("Q", "x", 0), ("C", "x", 1, 1, "s"),
-    ("T", "x", 2, 0), ("T", "x", 2, 1), ("W", 1), ("C", "x", 2, 0, "s"), ("Q", "x", 1), ("M1", 0),
-    ("C", "x", 2, 1, "s"), ("Q", "x", 2), ("T", "x", 3, 0), ("SQ", 0), ("T", "x", 3, 1), ("W", 1),
-    ("C", "x", 3, 0, "v"), ("M1", 1), ("C", "x", 3, 1, "s"), ("NV", 0), ("Q", "x", 3), ("CT", 0),
-    ("SQ", 1), ("T", "wb", 0, 0), ("CC", 0, "v"), ("T", "wb", 0, 1), ("CQ", 0), ("M1", 2),
-    ("CW", 0, "s"), ("NV", 1), ("CT", 1), ("Q", "wb", 0), ("SQ", 2), ("T", "wb", 1, 0),
-    ("CC", 1, "v"), ("T", "wb", 1, 1), ("M2", 0, 0), ("CW", 1, "s"), ("CQ", 1), ("NV", 2),
-    ("M1", 3), ("D", 0, 0, "v"), ("M2", 0, 1), ("SQ", 3), ("Q", "wb", 1), ("CT", 2),
-    ("T", "wb", 2, 0), ("D", 0, 1, "v"), ("CC", 2, "s"), ("M2", 1, 0), ("NV", 3), ("ST", 0, "A"),
-    ("M2", 1, 1), ("D", 1, 0, "s"), ("T", "wb", 2, 1), ("CQ", 2), ("D", 1, 1, "s"), ("CT", 3),
-    ("CW", 2, "v"), ("T", "wb", 3, 0), ("CC", 3, "s"), ("M2", 0, 2), ("ST", 1, "A"), ("M2", 1, 2),
-    ("D", 0, 2, "s"), ("CQ", 3), ("T", "wb", 3, 1), ("Q", "wb", 2), ("D", 1, 2, "s"), ("M2", 0, 3),
-    ("CW", 3, "v"), ("M2", 1, 3), ("D", 0, 3, "s"), ("M2", 2, 0), ("M2", 2, 1), ("D", 2, 0, "s"),
-    ("ST", 0, "B"), ("M2", 2, 2), ("D", 2, 1, "v"), ("M2", 2, 3), ("D", 2, 2, "s"),
-    ("T", "wb", 4, 0), ("D", 2, 3, "v"), ("T", "wb", 4, 1), ("D", 1, 3, "s"), ("Q", "wb", 3),
-    ("T", "wb", 5, 0), ("ST", 2, "W"), ("T", "wb", 5, 1), ("CW", 4, "s"), ("T", "wb", 6, 0),
-    ("CW", 5, "v"), ("M2", 3, 0), ("ST", 1, "B"), ("M2", 3, 1), ("D", 3, 0, "s"), ("M2", 3, 2),
-    ("D", 3, 1, "v"), ("M2", 3, 3), ("D", 3, 2, "s"), ("T", "wb", 6, 1), ("D", 3, 3, "v"),
-    ("T", "wb", 7, 0), ("CW", 6, "s"), ("T", "wb", 7, 1), ("Q", "wb", 4), ("ST", 3, "W"),
-    ("Q", "wb", 5), ("CW", 7, "s"), ("M2", 4, 0), ("Q", "wb", 6), ("M2", 4, 1), ("M2", 4, 2),
-    ("D", 4, 0, "v"), ("M2", 4, 3), ("D", 4, 1, "s"), ("M2", 5, 0), ("D", 4, 2, "v"), ("M2", 5, 1),
-    ("D", 4, 3, "s"), ("M2", 5, 2), ("D", 5, 0, "v"), ("M2", 5, 3), ("D", 5, 1, "s"),
-    ("ST", 4, "W"), ("M2", 6, 0), ("M2", 6, 1), ("D", 5, 2, "v"), ("D", 5, 3, "s"), ("M2", 6, 2),
-    ("M2", 6, 3), ("D", 6, 0, "v"), ("D", 6, 1, "s"), ("ST", 5, "W"), ("D", 6, 2, "v"),
-    ("D", 6, 3, "s"), ("Q", "wb", 7), ("M2", 7, 0), ("M2", 7, 1), ("D", 7, 0, "s"), ("M2", 7, 2),
-    ("D", 7, 1, "v"), ("M2", 7, 3), ("D", 7, 2, "s"), ("D", 7, 3, "v"), ("ST", 6, "W"),
+    ("W", 9), ("F", 0, "v"), ("F", 1, "v"), ("F", 2, "v"), ("T", "wa", 0, 0), ("T", "wa", 0, 1),
+    ("W", 1), ("C", "wa", 0, 0, "s"), ("T", "wa", 1, 0), ("C", "wa", 0, 1, "v"), ("T", "wa", 1, 1),
+    ("W", 1), ("G",), ("C", "wa", 1, 0, "v"), ("C", "wa", 1, 1, "s"), ("T", "wa", 2, 0),
+    ("Q", "wa", 0), ("GC",), ("T", "wa", 2, 1), ("W", 1), ("C", "wa", 2, 0, "s"), ("Q", "wa", 1),
+    ("T", "wa", 3, 0), ("C", "wa", 2, 1, "s"), ("T", "wa", 3, 1), ("W", 1), ("C", "wa", 3, 0, "s"),
+    ("C", "wa", 3, 1, "v"), ("T", "x", 0, 0), ("T", "x", 0, 1), ("W", 1), ("C", "x", 0, 0, "v"),
+    ("C", "x", 0, 1, "s"), ("T", "x", 1, 0), ("Q", "wa", 2), ("T", "x", 1, 1), ("W", 1),
+    ("C", "x", 1, 0, "s"), ("Q", "x", 0), ("T", "x", 2, 0), ("C", "x", 1, 1, "s"), ("Q", "wa", 3),
+    ("T", "x", 2, 1), ("W", 1), ("C", "x", 2, 0, "s"), ("Q", "x", 1), ("T", "x", 3, 0),
+    ("C", "x", 2, 1, "s"), ("T", "x", 3, 1), ("W", 1), ("C", "x", 3, 0, "s"), ("M1", 0),
+    ("C", "x", 3, 1, "v"), ("Q", "x", 3), ("M1", 1), ("Q", "x", 2), ("SQ", 0), ("T", "wb", 0, 0),
+    ("SQ", 1), ("NV", 0), ("T", "wb", 0, 1), ("T", "wb", 1, 0), ("CW", 0, "v"), ("T", "wb", 1, 1),
+    ("CT", 0), ("M1", 2), ("CW", 1, "s"), ("NV", 1), ("Q", "wb", 0), ("CC", 0, "s"),
+    ("T", "wb", 2, 0), ("CT", 1), ("SQ", 2), ("Q", "wb", 1), ("T", "wb", 2, 1), ("CC", 1, "v"),
+    ("M1", 3), ("CW", 2, "s"), ("CQ", 1), ("CQ", 0), ("NV", 2), ("M2", 0, 1), ("M2", 0, 0),
+    ("SQ", 3), ("Q", "wb", 2), ("M2", 1, 0), ("M2", 1, 1), ("CT", 2), ("D", 0, 0, "v"),
+    ("D", 0, 1, "s"), ("NV", 3), ("M2", 2, 1), ("D", 1, 1, "s"), ("ST", 0, "A"), ("T", "wb", 3, 0),
+    ("CC", 2, "s"), ("D", 1, 0, "v"), ("CT", 3), ("D", 2, 1, "s"), ("M2", 2, 0), ("CQ", 2),
+    ("ST", 1, "A"), ("CC", 3, "v"), ("T", "wb", 3, 1), ("D", 2, 0, "s"), ("CQ", 3), ("M2", 0, 2),
+    ("CW", 3, "v"), ("M2", 1, 2), ("M2", 0, 3), ("ST", 2, "A"), ("D", 0, 2, "s"), ("M2", 1, 3),
+    ("M2", 2, 3), ("D", 0, 3, "s"), ("T", "wb", 4, 0), ("D", 1, 3, "v"), ("D", 1, 2, "s"),
+    ("M2", 2, 2), ("Q", "wb", 3), ("ST", 0, "B"), ("T", "wb", 4, 1), ("D", 2, 3, "s"),
+    ("D", 2, 2, "v"), ("T", "wb", 5, 0), ("ST", 1, "B"), ("CW", 4, "s"), ("F", 3, "v"),
+    ("M2", 3, 2), ("F", 4, "v"), ("M2", 3, 0), ("M2", 3, 1), ("D", 3, 2, "v"), ("M2", 3, 3),
+    ("D", 3, 0, "s"), ("T", "wb", 5, 1), ("D", 3, 1, "v"), ("D", 3, 3, "s"), ("T", "wb", 6, 0),
+    ("Q", "wb", 4), ("ST", 2, "B"), ("T", "wb", 6, 1), ("CW", 5, "s"), ("T", "wb", 7, 0),
+    ("F", 5, "v"), ("T", "wb", 7, 1), ("CW", 6, "v"), ("ST", 3, "W"), ("M2", 4, 0), ("CW", 7, "s"),
+    ("M2", 4, 3), ("M2", 4, 1), ("D", 4, 0, "v"), ("M2", 4, 2), ("D", 4, 3, "s"), ("D", 4, 2, "v"),
+    ("D", 4, 1, "s"), ("Q", "wb", 5), ("Q", "wb", 6), ("ST", 4, "W"), ("F", 6, "v"), ("M2", 5, 0),
+    ("M2", 5, 3), ("Q", "wb", 7), ("M2", 5, 1), ("D", 5, 0, "s"), ("M2", 5, 2), ("M2", 6, 2),
+    ("D", 5, 1, "v"), ("D", 5, 3, "s"), ("M2", 6, 0), ("M2", 6, 3), ("D", 5, 2, "v"), ("M2", 6, 1),
+    ("D", 6, 0, "s"), ("M2", 7, 3), ("D", 6, 3, "v"), ("M2", 7, 1), ("D", 6, 1, "s"),
+    ("ST", 5, "W"), ("M2", 7, 2), ("D", 6, 2, "v"), ("M2", 7, 0), ("D", 7, 1, "s"),
+    ("D", 7, 0, "v"), ("D", 7, 2, "s"), ("ST", 6, "W"), ("F", 7, "v"), ("D", 7, 3, "s"),
     ("ST", 7, "W"),
 )
 

@@ -14,52 +14,22 @@ ALU = mybir.AluOpType
 ACT = mybir.ActivationFunctionType
 
 P = 128
+BATCH = 2
 D_MODEL = 2048
 LATENT = 512
 HEADS = 16
+NOPE = 128
 ROPE = 64
+K_PASS = 512
+PASSES = D_MODEL // K_PASS
+BANK = 512
+TILES = 4
+PAIRS = HEADS // 2
+SPLIT_PAIRS = 3
 EPS = 1e-6
 THETA = 10000.0
-FLOPS = 2 * 512 * D_MODEL * LATENT + 2 * 512 * LATENT * HEADS * 256
-
-
-ORDER = (
-    ("W", 9), ("F", 0, "v"), ("F", 1, "v"), ("F", 2, "v"), ("T", "wa", 0, 0), ("T", "wa", 0, 1),
-    ("W", 1), ("C", "wa", 0, 0, "s"), ("T", "wa", 1, 0), ("C", "wa", 0, 1, "v"), ("T", "wa", 1, 1),
-    ("W", 1), ("G",), ("C", "wa", 1, 0, "v"), ("C", "wa", 1, 1, "s"), ("T", "wa", 2, 0),
-    ("Q", "wa", 0), ("GC",), ("T", "wa", 2, 1), ("W", 1), ("C", "wa", 2, 0, "s"), ("Q", "wa", 1),
-    ("T", "wa", 3, 0), ("C", "wa", 2, 1, "s"), ("T", "wa", 3, 1), ("W", 1), ("C", "wa", 3, 0, "s"),
-    ("C", "wa", 3, 1, "v"), ("T", "x", 0, 0), ("T", "x", 0, 1), ("W", 1), ("C", "x", 0, 0, "v"),
-    ("C", "x", 0, 1, "s"), ("T", "x", 1, 0), ("Q", "wa", 2), ("T", "x", 1, 1), ("W", 1),
-    ("C", "x", 1, 0, "s"), ("Q", "x", 0), ("T", "x", 2, 0), ("C", "x", 1, 1, "s"), ("Q", "wa", 3),
-    ("T", "x", 2, 1), ("W", 1), ("C", "x", 2, 0, "s"), ("Q", "x", 1), ("T", "x", 3, 0),
-    ("C", "x", 2, 1, "s"), ("T", "x", 3, 1), ("W", 1), ("C", "x", 3, 0, "s"), ("M1", 0),
-    ("C", "x", 3, 1, "v"), ("Q", "x", 3), ("M1", 1), ("Q", "x", 2), ("SQ", 0), ("T", "wb", 0, 0),
-    ("SQ", 1), ("NV", 0), ("T", "wb", 0, 1), ("T", "wb", 1, 0), ("CW", 0, "v"), ("T", "wb", 1, 1),
-    ("CT", 0), ("M1", 2), ("CW", 1, "s"), ("NV", 1), ("Q", "wb", 0), ("CC", 0, "s"),
-    ("T", "wb", 2, 0), ("CT", 1), ("SQ", 2), ("Q", "wb", 1), ("T", "wb", 2, 1), ("CC", 1, "v"),
-    ("M1", 3), ("CW", 2, "s"), ("CQ", 1), ("CQ", 0), ("NV", 2), ("M2", 0, 1), ("M2", 0, 0),
-    ("SQ", 3), ("Q", "wb", 2), ("M2", 1, 0), ("M2", 1, 1), ("CT", 2), ("D", 0, 0, "v"),
-    ("D", 0, 1, "s"), ("NV", 3), ("M2", 2, 1), ("D", 1, 1, "s"), ("ST", 0, "A"), ("T", "wb", 3, 0),
-    ("CC", 2, "s"), ("D", 1, 0, "v"), ("CT", 3), ("D", 2, 1, "s"), ("M2", 2, 0), ("CQ", 2),
-    ("ST", 1, "A"), ("CC", 3, "v"), ("T", "wb", 3, 1), ("D", 2, 0, "s"), ("CQ", 3), ("M2", 0, 2),
-    ("CW", 3, "v"), ("M2", 1, 2), ("M2", 0, 3), ("ST", 2, "A"), ("D", 0, 2, "s"), ("M2", 1, 3),
-    ("M2", 2, 3), ("D", 0, 3, "s"), ("T", "wb", 4, 0), ("D", 1, 3, "v"), ("D", 1, 2, "s"),
-    ("M2", 2, 2), ("Q", "wb", 3), ("ST", 0, "B"), ("T", "wb", 4, 1), ("D", 2, 3, "s"),
-    ("D", 2, 2, "v"), ("T", "wb", 5, 0), ("ST", 1, "B"), ("CW", 4, "s"), ("F", 3, "v"),
-    ("M2", 3, 2), ("F", 4, "v"), ("M2", 3, 0), ("M2", 3, 1), ("D", 3, 2, "v"), ("M2", 3, 3),
-    ("D", 3, 0, "s"), ("T", "wb", 5, 1), ("D", 3, 1, "v"), ("D", 3, 3, "s"), ("T", "wb", 6, 0),
-    ("Q", "wb", 4), ("ST", 2, "B"), ("T", "wb", 6, 1), ("CW", 5, "s"), ("T", "wb", 7, 0),
-    ("F", 5, "v"), ("T", "wb", 7, 1), ("CW", 6, "v"), ("ST", 3, "W"), ("M2", 4, 0), ("CW", 7, "s"),
-    ("M2", 4, 3), ("M2", 4, 1), ("D", 4, 0, "v"), ("M2", 4, 2), ("D", 4, 3, "s"), ("D", 4, 2, "v"),
-    ("D", 4, 1, "s"), ("Q", "wb", 5), ("Q", "wb", 6), ("ST", 4, "W"), ("F", 6, "v"), ("M2", 5, 0),
-    ("M2", 5, 3), ("Q", "wb", 7), ("M2", 5, 1), ("D", 5, 0, "s"), ("M2", 5, 2), ("M2", 6, 2),
-    ("D", 5, 1, "v"), ("D", 5, 3, "s"), ("M2", 6, 0), ("M2", 6, 3), ("D", 5, 2, "v"), ("M2", 6, 1),
-    ("D", 6, 0, "s"), ("M2", 7, 3), ("D", 6, 3, "v"), ("M2", 7, 1), ("D", 6, 1, "s"),
-    ("ST", 5, "W"), ("M2", 7, 2), ("D", 6, 2, "v"), ("M2", 7, 0), ("D", 7, 1, "s"),
-    ("D", 7, 0, "v"), ("D", 7, 2, "s"), ("ST", 6, "W"), ("F", 7, "v"), ("D", 7, 3, "s"),
-    ("ST", 7, "W"),
-)
+WARM_START = 9
+FLOPS = 2 * BATCH * 256 * D_MODEL * LATENT + 2 * BATCH * 256 * LATENT * HEADS * 2 * NOPE
 
 
 def tile_modelnew_pb_kernel(
@@ -73,74 +43,76 @@ def tile_modelnew_pb_kernel(
         keep = ctx.enter_context(tc.tile_pool(name="keep", bufs=1))
         outs = ctx.enter_context(tc.tile_pool(name="outs", bufs=1))
         grp = ctx.enter_context(tc.tile_pool(name="grp", bufs=4))
-        work = ctx.enter_context(tc.tile_pool(name="work", bufs=4))
+        work = ctx.enter_context(tc.tile_pool(name="work", bufs=TILES))
         psum = ctx.enter_context(tc.psum_pool(name="psum", bufs=8))
 
-        kpe = const.tile([P, 4, ROPE], BF16)
-        for b in range(2):
+        kpe = const.tile([P, TILES, ROPE], BF16)
+        for b in range(BATCH):
             nc.scalar.dma_start(
-                out=kpe[b:P:2, :, :],
-                in_=k_pe_raw[b].rearrange("(q j) d -> q j d", j=4),
+                out=kpe[b:P:BATCH, :, :],
+                in_=k_pe_raw[b].rearrange("(q j) d -> q j d", j=TILES),
             )
-        ones_b = const.tile([P, P], BF16)
-        nc.vector.memset(ones_b[:], 1.0)
-        warm_rhs = const.tile([P, 512], BF16)
-        nc.vector.memset(warm_rhs[:], 0.0)
+        ones = const.tile([P, P], BF16)
+        nc.vector.memset(ones[:], 1.0)
+        zeros = const.tile([P, BANK], BF16)
+        nc.vector.memset(zeros[:], 0.0)
         gain_row = const.tile([P, LATENT], BF16)
         nc.vector.memset(gain_row[:], 0.0)
         nc.scalar.dma_start(
             out=gain_row[0:1, :], in_=kv_a_ln_w.rearrange("(o n) -> o n", o=1)
         )
 
-        raws = {}
+        loaded = {}
         wa_view = kv_a_w_ckv.rearrange("(u p e) k -> u e p k", u=2, e=2)
         for t in range(4):
-            wa_r = raw.tile([P, D_MODEL], BF16, name="wa_raw%d" % t)
-            nc.sync.dma_start(out=wa_r[:], in_=wa_view[t // 2, t % 2])
-            raws[("wa", t)] = wa_r
-        x_view = hidden_states.rearrange("b (q j) k -> b j q k", j=4)
-        for j in range(4):
-            x_r = raw.tile([P, D_MODEL], BF16, name="x_raw%d" % j)
-            for b in range(2):
-                nc.sync.dma_start(out=x_r[b:P:2, :], in_=x_view[b, j])
-            raws[("x", j)] = x_r
-        wb_view = kv_b_w.rearrange("(c p j) k -> c p (j k)", c=8, j=4)
-        for c in range(8):
-            wb_r = raw.tile([P, 4 * LATENT], BF16, name="wb_raw%d" % c)
-            nc.sync.dma_start(out=wb_r[:], in_=wb_view[c])
-            raws[("wb", c)] = wb_r
+            wa_raw = raw.tile([P, D_MODEL], BF16, name="wa_raw%d" % t)
+            nc.sync.dma_start(out=wa_raw[:], in_=wa_view[t // 2, t % 2])
+            loaded[("wa", t)] = wa_raw
+        x_view = hidden_states.rearrange("b (q j) k -> b j q k", j=TILES)
+        for j in range(TILES):
+            x_raw = raw.tile([P, D_MODEL], BF16, name="x_raw%d" % j)
+            for b in range(BATCH):
+                nc.sync.dma_start(out=x_raw[b:P:BATCH, :], in_=x_view[b, j])
+            loaded[("x", j)] = x_raw
+        wb_view = kv_b_w.rearrange("(c p i) k -> c p (i k)", c=PAIRS, i=4)
+        for c in range(PAIRS):
+            wb_raw = raw.tile([P, 4 * LATENT], BF16, name="wb_raw%d" % c)
+            nc.sync.dma_start(out=wb_raw[:], in_=wb_view[c])
+            loaded[("wb", c)] = wb_raw
 
-        twice_p = const.tile([P, 4], I32)
-        nc.gpsimd.iota(out=twice_p[:], pattern=[[0, 4]], base=0, channel_multiplier=2)
-        j_idx = const.tile([P, 4], I32)
-        nc.gpsimd.iota(out=j_idx[:], pattern=[[1, 4]], base=0, channel_multiplier=0)
-        ident_f = const.tile([P, P], F32)
-        make_identity(nc, ident_f[:])
-        ident_b = const.tile([P, P], BF16)
-        make_identity(nc, ident_b[:])
-        eps_t = const.tile([P, 1], F32)
-        nc.vector.memset(eps_t[:], EPS)
-        zero_t = const.tile([P, 1], F32)
-        nc.vector.memset(zero_t[:], 0.0)
+        twice_p = const.tile([P, TILES], I32)
+        nc.gpsimd.iota(out=twice_p[:], pattern=[[0, TILES]], base=0, channel_multiplier=2)
+        j_index = const.tile([P, TILES], I32)
+        nc.gpsimd.iota(out=j_index[:], pattern=[[1, TILES]], base=0, channel_multiplier=0)
+        ident_f32 = const.tile([P, P], F32)
+        make_identity(nc, ident_f32[:])
+        ident_bf16 = const.tile([P, P], BF16)
+        make_identity(nc, ident_bf16[:])
+        eps = const.tile([P, 1], F32)
+        nc.vector.memset(eps[:], EPS)
+        zero = const.tile([P, 1], F32)
+        nc.vector.memset(zero[:], 0.0)
 
-        warm_sin = const.tile([P, 1], F32)
-        nc.scalar.activation(out=warm_sin[:], in_=zero_t[:], func=ACT.Sin)
+        sin_first = const.tile([P, 1], F32)
+        nc.scalar.activation(out=sin_first[:], in_=zero[:], func=ACT.Sin)
 
-        four_q = const.tile([P, 4], I32)
+        four_q = const.tile([P, TILES], I32)
         nc.vector.tensor_single_scalar(
             out=four_q[:], in_=twice_p[:], scalar=0x1FC, op=ALU.bitwise_and
         )
-        pos = const.tile([P, 4], F32)
-        nc.vector.tensor_tensor(out=pos[:], in0=four_q[:], in1=j_idx[:], op=ALU.add)
-        turns = const.tile([P, 2, 4, 32], F32)
+        position = const.tile([P, TILES], F32)
+        nc.vector.tensor_tensor(
+            out=position[:], in0=four_q[:], in1=j_index[:], op=ALU.add
+        )
+        turns = const.tile([P, 2, TILES, ROPE // 2], F32)
         nc.vector.tensor_scalar(
             out=turns[:, 0, :, 0:1],
-            in0=pos[:].unsqueeze(2),
+            in0=position[:].unsqueeze(2),
             scalar1=1.0 / (2.0 * math.pi),
             scalar2=None,
             op0=ALU.mult,
         )
-        ratio = THETA ** (-1.0 / 32.0)
+        ratio = THETA ** (-2.0 / ROPE)
         for w in (1, 2, 4, 8, 16):
             nc.vector.tensor_scalar(
                 out=turns[:, 0, :, w : 2 * w],
@@ -152,274 +124,361 @@ def tile_modelnew_pb_kernel(
         nc.vector.tensor_scalar(
             out=turns[:, 1], in0=turns[:, 0], scalar1=0.25, scalar2=None, op0=ALU.add
         )
+        n_table = 2 * TILES * (ROPE // 2)
         turns_flat = turns[:].rearrange("p c j f -> p (c j f)")
-        whole_i = const.tile([P, 256], I32)
-        nc.vector.tensor_copy(out=whole_i[:], in_=turns_flat)
-        whole_f = const.tile([P, 256], F32)
-        nc.vector.tensor_copy(out=whole_f[:], in_=whole_i[:])
-        frac = const.tile([P, 256], F32)
+        whole_i32 = const.tile([P, n_table], I32)
+        nc.vector.tensor_copy(out=whole_i32[:], in_=turns_flat)
+        whole = const.tile([P, n_table], F32)
+        nc.vector.tensor_copy(out=whole[:], in_=whole_i32[:])
+        remainder = const.tile([P, n_table], F32)
         nc.vector.tensor_tensor(
-            out=frac[:], in0=turns_flat, in1=whole_f[:], op=ALU.subtract
+            out=remainder[:], in0=turns_flat, in1=whole[:], op=ALU.subtract
         )
-        neg_frac = const.tile([P, 256], F32)
+        less_turns = const.tile([P, n_table], F32)
         nc.vector.scalar_tensor_tensor(
-            out=neg_frac[:],
-            in0=frac[:],
+            out=less_turns[:],
+            in0=remainder[:],
             scalar=0.5,
-            in1=frac[:],
+            in1=remainder[:],
             op0=ALU.is_gt,
             op1=ALU.subtract,
         )
-        sincos = const.tile([P, 2, 4, 32], F32)
+        sin_cos = const.tile([P, 2, TILES, ROPE // 2], F32)
         nc.scalar.activation(
-            out=sincos[:].rearrange("p c j f -> p (c j f)"),
-            in_=neg_frac[:],
+            out=sin_cos[:].rearrange("p c j f -> p (c j f)"),
+            in_=less_turns[:],
             func=ACT.Sin,
             scale=-2.0 * math.pi,
         )
-        warm_sqrt = const.tile([P, 1], F32)
-        nc.scalar.activation(out=warm_sqrt[:], in_=eps_t[:], func=ACT.Sqrt)
+        sqrt_early = const.tile([P, 1], F32)
+        nc.scalar.activation(out=sqrt_early[:], in_=eps[:], func=ACT.Sqrt)
 
-        sin_t = sincos[:, 0]
-        cos_t = sincos[:, 1]
-        rope_a = const.tile([P, 4, ROPE], F32)
+        half = ROPE // 2
+        sin = sin_cos[:, 0]
+        cos = sin_cos[:, 1]
+        by_cos = const.tile([P, TILES, ROPE], F32)
         nc.vector.tensor_tensor(
-            out=rope_a[:].rearrange("p j (h f) -> p j h f", h=2),
+            out=by_cos[:].rearrange("p j (h f) -> p j h f", h=2),
             in0=kpe[:].rearrange("p j (h f) -> p j h f", h=2),
-            in1=cos_t.unsqueeze(2).to_broadcast([P, 4, 2, 32]),
+            in1=cos.unsqueeze(2).to_broadcast([P, TILES, 2, half]),
             op=ALU.mult,
         )
-        rope_b = const.tile([P, 4, ROPE], F32)
+        by_sin = const.tile([P, TILES, ROPE], F32)
         nc.vector.scalar_tensor_tensor(
-            out=rope_b[:, :, 0:32],
-            in0=kpe[:, :, 32:64],
+            out=by_sin[:, :, 0:half],
+            in0=kpe[:, :, half:ROPE],
             scalar=-1.0,
-            in1=sin_t,
+            in1=sin,
             op0=ALU.mult,
             op1=ALU.mult,
         )
         nc.vector.tensor_tensor(
-            out=rope_b[:, :, 32:64], in0=kpe[:, :, 0:32], in1=sin_t, op=ALU.mult
+            out=by_sin[:, :, half:ROPE], in0=kpe[:, :, 0:half], in1=sin, op=ALU.mult
         )
-        rope = const.tile([P, 4, ROPE], F32)
-        nc.vector.tensor_tensor(out=rope[:], in0=rope_a[:], in1=rope_b[:], op=ALU.add)
+        rotated = const.tile([P, TILES, ROPE], F32)
+        nc.vector.tensor_tensor(
+            out=rotated[:], in0=by_cos[:], in1=by_sin[:], op=ALU.add
+        )
 
-        gain_bc = const.tile([P, LATENT], F32)
+        wa_codes = keep.tile([P, PASSES, LATENT], U32, align_bytes=64)
+        wa_scales = keep.tile([P, PASSES, LATENT], U8, align_bytes=64)
+        x_codes = keep.tile([P, TILES, PASSES, P], U32, align_bytes=64)
+        x_scales = keep.tile([P, TILES, PASSES, P], U8, align_bytes=64)
+        n_codes = keep.tile([P, TILES, P], U32, align_bytes=64)
+        n_scales = keep.tile([P, TILES, P], U8, align_bytes=64)
+        wb_codes = keep.tile([P, PAIRS, BANK], U32, align_bytes=64)
+        wb_scales = keep.tile([P, PAIRS, BANK], U8, align_bytes=64)
 
-        wa_codes = keep.tile([P, 4, LATENT], U32, align_bytes=64)
-        wa_scales = keep.tile([P, 4, LATENT], U8, align_bytes=64)
-        x_codes = keep.tile([P, 4, 4, P], U32, align_bytes=64)
-        x_scales = keep.tile([P, 4, 4, P], U8, align_bytes=64)
-        c_codes = keep.tile([P, 4, P], U32, align_bytes=64)
-        c_scales = keep.tile([P, 4, P], U8, align_bytes=64)
-        wb_codes = keep.tile([P, 8, 512], U32, align_bytes=64)
-        wb_scales = keep.tile([P, 8, 512], U8, align_bytes=64)
-
-        key_view = out_0.rearrange("b h (q j) d -> b q h j d", j=4)
-        val_view = out_1.rearrange("b h (q j) d -> b q h j d", j=4)
+        gain_all = const.tile([P, LATENT], F32)
+        key_view = out_0.rearrange("b h (q j) d -> b q h j d", j=TILES)
+        value_view = out_1.rearrange("b h (q j) d -> b q h j d", j=TILES)
 
         live = {}
 
-        def copy_on(engine, out, in_):
-            if engine == "v":
-                nc.vector.tensor_copy(out=out, in_=in_)
-            else:
-                nc.scalar.copy(out=out, in_=in_)
+        def on_vector(out, in_):
+            nc.vector.tensor_copy(out=out, in_=in_)
 
-        def grouped_tile(kind, idx):
-            if ("g", kind, idx) not in live:
-                grouped = grp.tile([P, 4 * 512], BF16, tag="grouped", align_bytes=64)
-                live[("g", kind, idx)] = grouped
-            return live[("g", kind, idx)]
+        def on_scalar(out, in_):
+            nc.scalar.copy(out=out, in_=in_)
 
-        def out_tiles(c):
-            if ("key", c) not in live:
-                key_t = outs.tile([P, 2, 4, 192], F32, name="key%d" % c)
-                val_t = outs.tile([P, 2, 4, P], F32, name="val%d" % c)
-                live[("key", c)] = key_t
-                live[("val", c)] = val_t
-            return live[("key", c)], live[("val", c)]
-
-        for step in ORDER:
-            op = step[0]
-            if op == "W":
-                if "warm" not in live:
-                    warm_ps = psum.tile([P, 512], F32, tag="bank")
-                    live["warm"] = warm_ps
-                for rep in range(step[1]):
-                    nc.tensor.matmul(
-                        out=live["warm"][:], lhsT=ones_b[:], rhs=warm_rhs[:], start=True, stop=True
-                    )
-            elif op == "G":
-                gain_ps = psum.tile([P, LATENT], F32, tag="bank")
+        def keep_clock_up(count):
+            if "dummy" not in live:
+                dummy = psum.tile([P, BANK], F32, tag="bank")
+                live["dummy"] = dummy
+            for repeat in range(count):
                 nc.tensor.matmul(
-                    out=gain_ps[:], lhsT=ones_b[:], rhs=gain_row[:], start=True, stop=True
+                    out=live["dummy"][:], lhsT=ones[:], rhs=zeros[:], start=True, stop=True
                 )
-                live["gain_ps"] = gain_ps
-            elif op == "GC":
-                nc.vector.tensor_copy(
-                    out=gain_bc[:].rearrange("q (u e p) -> q u e p", u=2, e=2),
-                    in_=live["gain_ps"][:].rearrange("q (u p e) -> q u e p", u=2, e=2),
-                )
-            elif op == "T":
-                kind, idx, h = step[1], step[2], step[3]
-                words = raws[(kind, idx)][:].bitcast(F32)
-                bank = psum.tile([P, 512], F32, tag="bank")
+
+        def spread_gain():
+            gain_bank = psum.tile([P, LATENT], F32, tag="bank")
+            nc.tensor.matmul(
+                out=gain_bank[:], lhsT=ones[:], rhs=gain_row[:], start=True, stop=True
+            )
+            live["gain"] = gain_bank
+
+        def order_gain():
+            nc.vector.tensor_copy(
+                out=gain_all[:].rearrange("q (u e p) -> q u e p", u=2, e=2),
+                in_=live["gain"][:].rearrange("q (u p e) -> q u e p", u=2, e=2),
+            )
+
+        def transpose_pairs(what, index):
+            pairs = loaded[(what, index)][:].bitcast(F32)
+            for h in range(2):
+                bank = psum.tile([P, BANK], F32, tag="bank")
                 for m in range(4):
                     col = (4 * h + m) * P
                     nc.tensor.transpose(
                         out=bank[:, m * P : (m + 1) * P],
-                        in_=words[:, col : col + P],
-                        identity=ident_f[:],
+                        in_=pairs[:, col : col + P],
+                        identity=ident_f32[:],
                     )
-                live[("t", kind, idx, h)] = bank
-            elif op == "C":
-                kind, idx, h, engine = step[1], step[2], step[3], step[4]
-                view = (
-                    grouped_tile(kind, idx)[:]
-                    .bitcast(F32)
-                    .rearrange("q (g c u) -> q g c u", g=4, u=2)
-                )
-                copy_on(
-                    engine,
-                    view[:, 2 * h : 2 * h + 2],
-                    live[("t", kind, idx, h)][:].rearrange("q (g u c) -> q g c u", g=2, u=2),
-                )
-            elif op == "CW":
-                idx, engine = step[1], step[2]
-                view = (
-                    grouped_tile("wb", idx)[:]
-                    .bitcast(F32)
-                    .rearrange("q (p a m) -> q a p m", a=2, m=4)
-                )
-                for a in range(2):
-                    copy_on(
-                        engine,
-                        view[:, a],
-                        live[("t", "wb", idx, a)][:].rearrange("q (m p) -> q p m", m=4),
-                    )
-            elif op == "Q":
-                kind, idx = step[1], step[2]
-                grouped = live[("g", kind, idx)]
-                if kind == "wa":
-                    for g in range(4):
-                        nc.vector.quantize_mx(
-                            out=wa_codes[:, g, idx * P : (idx + 1) * P].bitcast(FP8X4),
-                            scales=wa_scales[:, g, idx * P : (idx + 1) * P],
-                            in_=grouped[:, g * 512 : (g + 1) * 512],
-                        )
-                elif kind == "x":
+                live[("bank", what, index, h)] = bank
+
+        def grouped_tile(what, index):
+            if ("grouped", what, index) not in live:
+                grouped = grp.tile([P, 4 * BANK], BF16, tag="grouped", align_bytes=64)
+                live[("grouped", what, index)] = grouped
+            return live[("grouped", what, index)]
+
+        def regroup(what, index, h, copy):
+            view = (
+                grouped_tile(what, index)[:]
+                .bitcast(F32)
+                .rearrange("q (g r u) -> q g r u", g=PASSES, u=2)
+            )
+            copy(
+                view[:, 2 * h : 2 * h + 2],
+                live[("bank", what, index, h)][:].rearrange("q (g u r) -> q g r u", g=2, u=2),
+            )
+
+        def regroup_rows(c, copy):
+            view = (
+                grouped_tile("wb", c)[:]
+                .bitcast(F32)
+                .rearrange("q (p a m) -> q a p m", a=2, m=4)
+            )
+            for a in range(2):
+                copy(view[:, a], live[("bank", "wb", c, a)][:].rearrange("q (m p) -> q p m", m=4))
+
+        def quantise(what, index):
+            grouped = live[("grouped", what, index)]
+            if what == "wa":
+                rows = slice(index * P, (index + 1) * P)
+                for g in range(PASSES):
                     nc.vector.quantize_mx(
-                        out=x_codes[:, idx].rearrange("q g c -> q (g c)").bitcast(FP8X4),
-                        scales=x_scales[:, idx].rearrange("q g c -> q (g c)"),
-                        in_=grouped[:],
+                        out=wa_codes[:, g, rows].bitcast(FP8X4),
+                        scales=wa_scales[:, g, rows],
+                        in_=grouped[:, g * 4 * P : (g + 1) * 4 * P],
                     )
-                else:
-                    nc.vector.quantize_mx(
-                        out=wb_codes[:, idx, :].bitcast(FP8X4),
-                        scales=wb_scales[:, idx, :],
-                        in_=grouped[:],
-                    )
-            elif op == "M1":
-                j = step[1]
-                acc = psum.tile([P, LATENT], F32, tag="bank")
-                for g in range(4):
-                    nc.tensor.matmul_mx(
-                        out=acc[:],
-                        lhsT=x_codes[:, j, g, :].bitcast(FP8X4),
-                        lhsT_scale=x_scales[:, j, g, :],
-                        rhs=wa_codes[:, g, :].bitcast(FP8X4),
-                        rhs_scale=wa_scales[:, g, :],
-                        start=(g == 0),
-                        stop=(g == 3),
-                    )
-                live[("acc", j)] = acc
-            elif op == "SQ":
-                j = step[1]
-                squares = work.tile([P, LATENT], BF16, tag="squares")
-                ssq = work.tile([P, 1], F32, tag="ssq")
-                nc.scalar.activation(
-                    out=squares[:], in_=live[("acc", j)][:], func=ACT.Square, accum_out=ssq[:]
-                )
-                std = work.tile([P, 1], F32, tag="std")
-                nc.scalar.activation(
-                    out=std[:], in_=ssq[:], func=ACT.Sqrt, bias=eps_t[:], scale=1.0 / LATENT
-                )
-                live[("std", j)] = std
-            elif op == "NV":
-                j = step[1]
-                rstd = work.tile([P, 1], F32, tag="rstd")
-                nc.vector.reciprocal(out=rstd[:], in_=live[("std", j)][:])
-                normed = work.tile([P, LATENT], BF16, tag="normed")
-                nc.vector.scalar_tensor_tensor(
-                    out=normed[:],
-                    in0=live[("acc", j)][:],
-                    scalar=rstd[:],
-                    in1=gain_bc[:],
-                    op0=ALU.mult,
-                    op1=ALU.mult,
-                )
-                live[("normed", j)] = normed
-            elif op == "CT":
-                j = step[1]
-                bank = psum.tile([P, 4, P], BF16, tag="bank")
-                for t in range(4):
-                    nc.tensor.transpose(
-                        out=bank[:, t, :],
-                        in_=live[("normed", j)][:, t * P : (t + 1) * P],
-                        identity=ident_b[:],
-                    )
-                live[("ct", j)] = bank
-            elif op == "CC":
-                j, engine = step[1], step[2]
-                cgrouped = work.tile([P, P, 4], BF16, tag="cgrouped", align_bytes=64)
-                copy_on(engine, cgrouped[:], live[("ct", j)][:].rearrange("q t c -> q c t"))
-                live[("cg", j)] = cgrouped
-            elif op == "CQ":
-                j = step[1]
+            elif what == "x":
                 nc.vector.quantize_mx(
-                    out=c_codes[:, j, :].bitcast(FP8X4),
-                    scales=c_scales[:, j, :],
-                    in_=live[("cg", j)][:].rearrange("q c t -> q (c t)"),
+                    out=x_codes[:, index].rearrange("q g r -> q (g r)").bitcast(FP8X4),
+                    scales=x_scales[:, index].rearrange("q g r -> q (g r)"),
+                    in_=grouped[:],
                 )
-            elif op == "F":
-                c, engine = step[1], step[2]
-                key_t, val_t = out_tiles(c)
-                copy_on(
-                    engine,
-                    key_t[:, :, :, P:192],
-                    rope[:].unsqueeze(1).to_broadcast([P, 2, 4, ROPE]),
-                )
-            elif op == "M2":
-                c, j = step[1], step[2]
-                acc = psum.tile([P, 512], F32, tag="bank")
-                nc.tensor.matmul_mx(
-                    out=acc[:],
-                    lhsT=c_codes[:, j, :].bitcast(FP8X4),
-                    lhsT_scale=c_scales[:, j, :],
-                    rhs=wb_codes[:, c, :].bitcast(FP8X4),
-                    rhs_scale=wb_scales[:, c, :],
-                    start=True,
-                    stop=True,
-                )
-                live[("o", c, j)] = acc
-            elif op == "D":
-                c, j, engine = step[1], step[2], step[3]
-                key_t, val_t = out_tiles(c)
-                parts = live[("o", c, j)][:].rearrange("p (h s d) -> p h s d", h=2, s=2)
-                copy_on(engine, key_t[:, :, j, 0:P], parts[:, :, 0, :])
-                copy_on(engine, val_t[:, :, j, :], parts[:, :, 1, :])
             else:
-                assert op == "ST"
-                c, part = step[1], step[2]
-                key_t, val_t = out_tiles(c)
-                j0, j1 = {"A": (0, 2), "B": (2, 4), "W": (0, 4)}[part]
-                for b in range(2):
-                    nc.sync.dma_start(
-                        out=key_view[b, :, 2 * c : 2 * c + 2, j0:j1, :],
-                        in_=key_t[b:P:2, :, j0:j1, :],
-                    )
-                    nc.sync.dma_start(
-                        out=val_view[b, :, 2 * c : 2 * c + 2, j0:j1, :],
-                        in_=val_t[b:P:2, :, j0:j1, :],
-                    )
+                nc.vector.quantize_mx(
+                    out=wb_codes[:, index, :].bitcast(FP8X4),
+                    scales=wb_scales[:, index, :],
+                    in_=grouped[:],
+                )
+
+        def first_matmul(j):
+            ckv = psum.tile([P, LATENT], F32, tag="bank")
+            for g in range(PASSES):
+                nc.tensor.matmul_mx(
+                    out=ckv[:],
+                    lhsT=x_codes[:, j, g, :].bitcast(FP8X4),
+                    lhsT_scale=x_scales[:, j, g, :],
+                    rhs=wa_codes[:, g, :].bitcast(FP8X4),
+                    rhs_scale=wa_scales[:, g, :],
+                    start=(g == 0),
+                    stop=(g == PASSES - 1),
+                )
+            live[("ckv", j)] = ckv
+
+        def root_mean_square(j):
+            squares = work.tile([P, LATENT], BF16, tag="squares")
+            sum_squares = work.tile([P, 1], F32, tag="sum_squares")
+            nc.scalar.activation(
+                out=squares[:], in_=live[("ckv", j)][:], func=ACT.Square, accum_out=sum_squares[:]
+            )
+            rms = work.tile([P, 1], F32, tag="rms")
+            nc.scalar.activation(
+                out=rms[:], in_=sum_squares[:], func=ACT.Sqrt, bias=eps[:], scale=1.0 / LATENT
+            )
+            live[("rms", j)] = rms
+
+        def normalise(j):
+            inverse = work.tile([P, 1], F32, tag="inverse")
+            nc.vector.reciprocal(out=inverse[:], in_=live[("rms", j)][:])
+            normed = work.tile([P, LATENT], BF16, tag="normed")
+            nc.vector.scalar_tensor_tensor(
+                out=normed[:],
+                in0=live[("ckv", j)][:],
+                scalar=inverse[:],
+                in1=gain_all[:],
+                op0=ALU.mult,
+                op1=ALU.mult,
+            )
+            live[("normed", j)] = normed
+
+        def transpose_normed(j):
+            bank = psum.tile([P, 4, P], BF16, tag="bank")
+            for t in range(4):
+                nc.tensor.transpose(
+                    out=bank[:, t, :],
+                    in_=live[("normed", j)][:, t * P : (t + 1) * P],
+                    identity=ident_bf16[:],
+                )
+            live[("bank", "normed", j)] = bank
+
+        def regroup_normed(j, copy):
+            grouped = work.tile([P, P, 4], BF16, tag="grouped_normed", align_bytes=64)
+            copy(grouped[:], live[("bank", "normed", j)][:].rearrange("q t r -> q r t"))
+            live[("grouped", "normed", j)] = grouped
+
+        def quantise_normed(j):
+            nc.vector.quantize_mx(
+                out=n_codes[:, j, :].bitcast(FP8X4),
+                scales=n_scales[:, j, :],
+                in_=live[("grouped", "normed", j)][:].rearrange("q r t -> q (r t)"),
+            )
+
+        def fill_rotated(c):
+            key = outs.tile([P, 2, TILES, NOPE + ROPE], F32, name="key%d" % c)
+            value = outs.tile([P, 2, TILES, NOPE], F32, name="value%d" % c)
+            live[("key", c)] = key
+            live[("value", c)] = value
+            nc.vector.tensor_copy(
+                out=key[:, :, :, NOPE : NOPE + ROPE],
+                in_=rotated[:].unsqueeze(1).to_broadcast([P, 2, TILES, ROPE]),
+            )
+
+        def second_matmul(c, j):
+            kv = psum.tile([P, BANK], F32, tag="bank")
+            nc.tensor.matmul_mx(
+                out=kv[:],
+                lhsT=n_codes[:, j, :].bitcast(FP8X4),
+                lhsT_scale=n_scales[:, j, :],
+                rhs=wb_codes[:, c, :].bitcast(FP8X4),
+                rhs_scale=wb_scales[:, c, :],
+                start=True,
+                stop=True,
+            )
+            live[("kv", c, j)] = kv
+
+        def copy_out(c, j, copy):
+            parts = live[("kv", c, j)][:].rearrange("p (h s d) -> p h s d", h=2, s=2)
+            copy(live[("key", c)][:, :, j, 0:NOPE], parts[:, :, 0, :])
+            copy(live[("value", c)][:, :, j, :], parts[:, :, 1, :])
+
+        def store(c, j0, j1):
+            heads = slice(2 * c, 2 * c + 2)
+            for b in range(BATCH):
+                nc.sync.dma_start(
+                    out=key_view[b, :, heads, j0:j1, :],
+                    in_=live[("key", c)][b:P:BATCH, :, j0:j1, :],
+                )
+                nc.sync.dma_start(
+                    out=value_view[b, :, heads, j0:j1, :],
+                    in_=live[("value", c)][b:P:BATCH, :, j0:j1, :],
+                )
+
+        keep_clock_up(WARM_START)
+        for c in range(SPLIT_PAIRS):
+            fill_rotated(c)
+        arrivals = (
+            ("wa", 0), ("wa", 1), ("wa", 2), ("wa", 3), ("x", 0), ("x", 1), ("x", 2), ("x", 3),
+        )
+        for n, (what, index) in enumerate(arrivals):
+            transpose_pairs(what, index)
+            keep_clock_up(1)
+            if n == 1:
+                spread_gain()
+            regroup(what, index, 0, on_scalar)
+            regroup(what, index, 1, on_vector if n % 2 == 0 else on_scalar)
+            if n > 0:
+                quantise(*arrivals[n - 1])
+            if n == 1:
+                order_gain()
+
+        first_matmul(0)
+        quantise("x", 3)
+        first_matmul(1)
+        root_mean_square(0)
+        transpose_pairs("wb", 0)
+        root_mean_square(1)
+        normalise(0)
+        transpose_pairs("wb", 1)
+        regroup_rows(0, on_vector)
+        transpose_normed(0)
+        first_matmul(2)
+        regroup_rows(1, on_scalar)
+        normalise(1)
+        quantise("wb", 0)
+        regroup_normed(0, on_scalar)
+        transpose_normed(1)
+        transpose_pairs("wb", 2)
+        root_mean_square(2)
+        quantise("wb", 1)
+        regroup_normed(1, on_vector)
+        first_matmul(3)
+        regroup_rows(2, on_scalar)
+        quantise_normed(0)
+        quantise_normed(1)
+        normalise(2)
+        second_matmul(0, 0)
+        second_matmul(0, 1)
+        root_mean_square(3)
+        quantise("wb", 2)
+        second_matmul(1, 0)
+        second_matmul(1, 1)
+        transpose_normed(2)
+        copy_out(0, 0, on_vector)
+        copy_out(0, 1, on_scalar)
+        store(0, 0, 2)
+        normalise(3)
+        second_matmul(2, 0)
+        second_matmul(2, 1)
+        copy_out(1, 1, on_scalar)
+        copy_out(1, 0, on_vector)
+        store(1, 0, 2)
+        regroup_normed(2, on_scalar)
+        transpose_normed(3)
+        transpose_pairs("wb", 3)
+        quantise_normed(2)
+        copy_out(2, 0, on_scalar)
+        copy_out(2, 1, on_scalar)
+        store(2, 0, 2)
+        regroup_normed(3, on_vector)
+        quantise_normed(3)
+        for c in range(SPLIT_PAIRS):
+            second_matmul(c, 2)
+            second_matmul(c, 3)
+        regroup_rows(3, on_vector)
+        copy_out(0, 2, on_scalar)
+        copy_out(0, 3, on_scalar)
+        store(0, 2, 4)
+        copy_out(1, 3, on_vector)
+        copy_out(1, 2, on_scalar)
+        store(1, 2, 4)
+        quantise("wb", 3)
+        copy_out(2, 3, on_scalar)
+        copy_out(2, 2, on_vector)
+        store(2, 2, 4)
+
+        for c in range(SPLIT_PAIRS, PAIRS):
+            if c + 1 < PAIRS:
+                transpose_pairs("wb", c + 1)
+                regroup_rows(c + 1, on_scalar)
+            fill_rotated(c)
+            for j in range(TILES):
+                second_matmul(c, j)
+            for j in range(TILES):
+                copy_out(c, j, on_vector if j % 2 == 0 else on_scalar)
+            store(c, 0, TILES)
+            if c + 1 < PAIRS:
+                quantise("wb", c + 1)

import math
from contextlib import ExitStack

import concourse.mybir as mybir
from concourse.masks import make_identity

F32 = mybir.dt.float32
BF16 = mybir.dt.bfloat16
I32 = mybir.dt.int32
U32 = mybir.dt.uint32
U8 = mybir.dt.uint8
FP8X4 = mybir.dt.float8_e4m3fn_x4
ALU = mybir.AluOpType
ACT = mybir.ActivationFunctionType

P = 128
BATCH = 2
D_MODEL = 2048
LATENT = 512
HEADS = 16
NOPE = 128
ROPE = 64
K_PASS = 512
PASSES = D_MODEL // K_PASS
BANK = 512
TILES = 4
PAIRS = HEADS // 2
SPLIT_PAIRS = 3
EPS = 1e-6
THETA = 10000.0
WARM_START = 9
FLOPS = 2 * BATCH * 256 * D_MODEL * LATENT + 2 * BATCH * 256 * LATENT * HEADS * 2 * NOPE


def tile_modelnew_pb_kernel(
    tc, hidden_states, kv_a_w_ckv, k_pe_raw, kv_a_ln_w, kv_b_w, out_0, out_1
):
    nc = tc.nc
    with ExitStack() as ctx:
        ctx.enter_context(tc.manual_schedule())
        const = ctx.enter_context(tc.tile_pool(name="const", bufs=1))
        raw = ctx.enter_context(tc.tile_pool(name="raw", bufs=1))
        keep = ctx.enter_context(tc.tile_pool(name="keep", bufs=1))
        outs = ctx.enter_context(tc.tile_pool(name="outs", bufs=1))
        grp = ctx.enter_context(tc.tile_pool(name="grp", bufs=4))
        work = ctx.enter_context(tc.tile_pool(name="work", bufs=TILES))
        psum = ctx.enter_context(tc.psum_pool(name="psum", bufs=8))

        kpe = const.tile([P, TILES, ROPE], BF16)
        for b in range(BATCH):
            nc.scalar.dma_start(
                out=kpe[b:P:BATCH, :, :],
                in_=k_pe_raw[b].rearrange("(q j) d -> q j d", j=TILES),
            )
        ones = const.tile([P, P], BF16)
        nc.vector.memset(ones[:], 1.0)
        zeros = const.tile([P, BANK], BF16)
        nc.vector.memset(zeros[:], 0.0)
        gain_row = const.tile([P, LATENT], BF16)
        nc.vector.memset(gain_row[:], 0.0)
        nc.scalar.dma_start(
            out=gain_row[0:1, :], in_=kv_a_ln_w.rearrange("(o n) -> o n", o=1)
        )

        loaded = {}
        wa_view = kv_a_w_ckv.rearrange("(u p e) k -> u e p k", u=2, e=2)
        for t in range(4):
            wa_raw = raw.tile([P, D_MODEL], BF16, name="wa_raw%d" % t)
            nc.sync.dma_start(out=wa_raw[:], in_=wa_view[t // 2, t % 2])
            loaded[("wa", t)] = wa_raw
        x_view = hidden_states.rearrange("b (q j) k -> b j q k", j=TILES)
        for j in range(TILES):
            x_raw = raw.tile([P, D_MODEL], BF16, name="x_raw%d" % j)
            for b in range(BATCH):
                nc.sync.dma_start(out=x_raw[b:P:BATCH, :], in_=x_view[b, j])
            loaded[("x", j)] = x_raw
        wb_view = kv_b_w.rearrange("(c p i) k -> c p (i k)", c=PAIRS, i=4)
        for c in range(PAIRS):
            wb_raw = raw.tile([P, 4 * LATENT], BF16, name="wb_raw%d" % c)
            nc.sync.dma_start(out=wb_raw[:], in_=wb_view[c])
            loaded[("wb", c)] = wb_raw

        twice_p = const.tile([P, TILES], I32)
        nc.gpsimd.iota(out=twice_p[:], pattern=[[0, TILES]], base=0, channel_multiplier=2)
        j_index = const.tile([P, TILES], I32)
        nc.gpsimd.iota(out=j_index[:], pattern=[[1, TILES]], base=0, channel_multiplier=0)
        ident_f32 = const.tile([P, P], F32)
        make_identity(nc, ident_f32[:])
        ident_bf16 = const.tile([P, P], BF16)
        make_identity(nc, ident_bf16[:])
        eps = const.tile([P, 1], F32)
        nc.vector.memset(eps[:], EPS)
        zero = const.tile([P, 1], F32)
        nc.vector.memset(zero[:], 0.0)

        sin_first = const.tile([P, 1], F32)
        nc.scalar.activation(out=sin_first[:], in_=zero[:], func=ACT.Sin)

        four_q = const.tile([P, TILES], I32)
        nc.vector.tensor_single_scalar(
            out=four_q[:], in_=twice_p[:], scalar=0x1FC, op=ALU.bitwise_and
        )
        position = const.tile([P, TILES], F32)
        nc.vector.tensor_tensor(
            out=position[:], in0=four_q[:], in1=j_index[:], op=ALU.add
        )
        turns = const.tile([P, 2, TILES, ROPE // 2], F32)
        nc.vector.tensor_scalar(
            out=turns[:, 0, :, 0:1],
            in0=position[:].unsqueeze(2),
            scalar1=1.0 / (2.0 * math.pi),
            scalar2=None,
            op0=ALU.mult,
        )
        ratio = THETA ** (-2.0 / ROPE)
        for w in (1, 2, 4, 8, 16):
            nc.vector.tensor_scalar(
                out=turns[:, 0, :, w : 2 * w],
                in0=turns[:, 0, :, 0:w],
                scalar1=ratio**w,
                scalar2=None,
                op0=ALU.mult,
            )
        nc.vector.tensor_scalar(
            out=turns[:, 1], in0=turns[:, 0], scalar1=0.25, scalar2=None, op0=ALU.add
        )
        n_table = 2 * TILES * (ROPE // 2)
        turns_flat = turns[:].rearrange("p c j f -> p (c j f)")
        whole_i32 = const.tile([P, n_table], I32)
        nc.vector.tensor_copy(out=whole_i32[:], in_=turns_flat)
        whole = const.tile([P, n_table], F32)
        nc.vector.tensor_copy(out=whole[:], in_=whole_i32[:])
        remainder = const.tile([P, n_table], F32)
        nc.vector.tensor_tensor(
            out=remainder[:], in0=turns_flat, in1=whole[:], op=ALU.subtract
        )
        less_turns = const.tile([P, n_table], F32)
        nc.vector.scalar_tensor_tensor(
            out=less_turns[:],
            in0=remainder[:],
            scalar=0.5,
            in1=remainder[:],
            op0=ALU.is_gt,
            op1=ALU.subtract,
        )
        sin_cos = const.tile([P, 2, TILES, ROPE // 2], F32)
        nc.scalar.activation(
            out=sin_cos[:].rearrange("p c j f -> p (c j f)"),
            in_=less_turns[:],
            func=ACT.Sin,
            scale=-2.0 * math.pi,
        )
        sqrt_early = const.tile([P, 1], F32)
        nc.scalar.activation(out=sqrt_early[:], in_=eps[:], func=ACT.Sqrt)

        half = ROPE // 2
        sin = sin_cos[:, 0]
        cos = sin_cos[:, 1]
        by_cos = const.tile([P, TILES, ROPE], F32)
        nc.vector.tensor_tensor(
            out=by_cos[:].rearrange("p j (h f) -> p j h f", h=2),
            in0=kpe[:].rearrange("p j (h f) -> p j h f", h=2),
            in1=cos.unsqueeze(2).to_broadcast([P, TILES, 2, half]),
            op=ALU.mult,
        )
        by_sin = const.tile([P, TILES, ROPE], F32)
        nc.vector.scalar_tensor_tensor(
            out=by_sin[:, :, 0:half],
            in0=kpe[:, :, half:ROPE],
            scalar=-1.0,
            in1=sin,
            op0=ALU.mult,
            op1=ALU.mult,
        )
        nc.vector.tensor_tensor(
            out=by_sin[:, :, half:ROPE], in0=kpe[:, :, 0:half], in1=sin, op=ALU.mult
        )
        rotated = const.tile([P, TILES, ROPE], F32)
        nc.vector.tensor_tensor(
            out=rotated[:], in0=by_cos[:], in1=by_sin[:], op=ALU.add
        )

        wa_codes = keep.tile([P, PASSES, LATENT], U32, align_bytes=64)
        wa_scales = keep.tile([P, PASSES, LATENT], U8, align_bytes=64)
        x_codes = keep.tile([P, TILES, PASSES, P], U32, align_bytes=64)
        x_scales = keep.tile([P, TILES, PASSES, P], U8, align_bytes=64)
        n_codes = keep.tile([P, TILES, P], U32, align_bytes=64)
        n_scales = keep.tile([P, TILES, P], U8, align_bytes=64)
        wb_codes = keep.tile([P, PAIRS, BANK], U32, align_bytes=64)
        wb_scales = keep.tile([P, PAIRS, BANK], U8, align_bytes=64)

        gain_all = const.tile([P, LATENT], F32)
        key_view = out_0.rearrange("b h (q j) d -> b q h j d", j=TILES)
        value_view = out_1.rearrange("b h (q j) d -> b q h j d", j=TILES)

        live = {}

        def on_vector(out, in_):
            nc.vector.tensor_copy(out=out, in_=in_)

        def on_scalar(out, in_):
            nc.scalar.copy(out=out, in_=in_)

        def keep_clock_up(count):
            if "dummy" not in live:
                dummy = psum.tile([P, BANK], F32, tag="bank")
                live["dummy"] = dummy
            for repeat in range(count):
                nc.tensor.matmul(
                    out=live["dummy"][:], lhsT=ones[:], rhs=zeros[:], start=True, stop=True
                )

        def spread_gain():
            gain_bank = psum.tile([P, LATENT], F32, tag="bank")
            nc.tensor.matmul(
                out=gain_bank[:], lhsT=ones[:], rhs=gain_row[:], start=True, stop=True
            )
            live["gain"] = gain_bank

        def order_gain():
            nc.vector.tensor_copy(
                out=gain_all[:].rearrange("q (u e p) -> q u e p", u=2, e=2),
                in_=live["gain"][:].rearrange("q (u p e) -> q u e p", u=2, e=2),
            )

        def transpose_pairs(what, index):
            pairs = loaded[(what, index)][:].bitcast(F32)
            for h in range(2):
                bank = psum.tile([P, BANK], F32, tag="bank")
                for m in range(4):
                    col = (4 * h + m) * P
                    nc.tensor.transpose(
                        out=bank[:, m * P : (m + 1) * P],
                        in_=pairs[:, col : col + P],
                        identity=ident_f32[:],
                    )
                live[("bank", what, index, h)] = bank

        def grouped_tile(what, index):
            if ("grouped", what, index) not in live:
                grouped = grp.tile([P, 4 * BANK], BF16, tag="grouped", align_bytes=64)
                live[("grouped", what, index)] = grouped
            return live[("grouped", what, index)]

        def regroup(what, index, h, copy):
            view = (
                grouped_tile(what, index)[:]
                .bitcast(F32)
                .rearrange("q (g r u) -> q g r u", g=PASSES, u=2)
            )
            copy(
                view[:, 2 * h : 2 * h + 2],
                live[("bank", what, index, h)][:].rearrange("q (g u r) -> q g r u", g=2, u=2),
            )

        def regroup_rows(c, copy):
            view = (
                grouped_tile("wb", c)[:]
                .bitcast(F32)
                .rearrange("q (p a m) -> q a p m", a=2, m=4)
            )
            for a in range(2):
                copy(view[:, a], live[("bank", "wb", c, a)][:].rearrange("q (m p) -> q p m", m=4))

        def quantise(what, index):
            grouped = live[("grouped", what, index)]
            if what == "wa":
                rows = slice(index * P, (index + 1) * P)
                for g in range(PASSES):
                    nc.vector.quantize_mx(
                        out=wa_codes[:, g, rows].bitcast(FP8X4),
                        scales=wa_scales[:, g, rows],
                        in_=grouped[:, g * 4 * P : (g + 1) * 4 * P],
                    )
            elif what == "x":
                nc.vector.quantize_mx(
                    out=x_codes[:, index].rearrange("q g r -> q (g r)").bitcast(FP8X4),
                    scales=x_scales[:, index].rearrange("q g r -> q (g r)"),
                    in_=grouped[:],
                )
            else:
                nc.vector.quantize_mx(
                    out=wb_codes[:, index, :].bitcast(FP8X4),
                    scales=wb_scales[:, index, :],
                    in_=grouped[:],
                )

        def first_matmul(j):
            ckv = psum.tile([P, LATENT], F32, tag="bank")
            for g in range(PASSES):
                nc.tensor.matmul_mx(
                    out=ckv[:],
                    lhsT=x_codes[:, j, g, :].bitcast(FP8X4),
                    lhsT_scale=x_scales[:, j, g, :],
                    rhs=wa_codes[:, g, :].bitcast(FP8X4),
                    rhs_scale=wa_scales[:, g, :],
                    start=(g == 0),
                    stop=(g == PASSES - 1),
                )
            live[("ckv", j)] = ckv

        def root_mean_square(j):
            squares = work.tile([P, LATENT], BF16, tag="squares")
            sum_squares = work.tile([P, 1], F32, tag="sum_squares")
            nc.scalar.activation(
                out=squares[:], in_=live[("ckv", j)][:], func=ACT.Square, accum_out=sum_squares[:]
            )
            rms = work.tile([P, 1], F32, tag="rms")
            nc.scalar.activation(
                out=rms[:], in_=sum_squares[:], func=ACT.Sqrt, bias=eps[:], scale=1.0 / LATENT
            )
            live[("rms", j)] = rms

        def normalise(j):
            inverse = work.tile([P, 1], F32, tag="inverse")
            nc.vector.reciprocal(out=inverse[:], in_=live[("rms", j)][:])
            normed = work.tile([P, LATENT], BF16, tag="normed")
            nc.vector.scalar_tensor_tensor(
                out=normed[:],
                in0=live[("ckv", j)][:],
                scalar=inverse[:],
                in1=gain_all[:],
                op0=ALU.mult,
                op1=ALU.mult,
            )
            live[("normed", j)] = normed

        def transpose_normed(j):
            bank = psum.tile([P, 4, P], BF16, tag="bank")
            for t in range(4):
                nc.tensor.transpose(
                    out=bank[:, t, :],
                    in_=live[("normed", j)][:, t * P : (t + 1) * P],
                    identity=ident_bf16[:],
                )
            live[("bank", "normed", j)] = bank

        def regroup_normed(j, copy):
            grouped = work.tile([P, P, 4], BF16, tag="grouped_normed", align_bytes=64)
            copy(grouped[:], live[("bank", "normed", j)][:].rearrange("q t r -> q r t"))
            live[("grouped", "normed", j)] = grouped

        def quantise_normed(j):
            nc.vector.quantize_mx(
                out=n_codes[:, j, :].bitcast(FP8X4),
                scales=n_scales[:, j, :],
                in_=live[("grouped", "normed", j)][:].rearrange("q r t -> q (r t)"),
            )

        def fill_rotated(c):
            key = outs.tile([P, 2, TILES, NOPE + ROPE], F32, name="key%d" % c)
            value = outs.tile([P, 2, TILES, NOPE], F32, name="value%d" % c)
            live[("key", c)] = key
            live[("value", c)] = value
            nc.vector.tensor_copy(
                out=key[:, :, :, NOPE : NOPE + ROPE],
                in_=rotated[:].unsqueeze(1).to_broadcast([P, 2, TILES, ROPE]),
            )

        def second_matmul(c, j):
            kv = psum.tile([P, BANK], F32, tag="bank")
            nc.tensor.matmul_mx(
                out=kv[:],
                lhsT=n_codes[:, j, :].bitcast(FP8X4),
                lhsT_scale=n_scales[:, j, :],
                rhs=wb_codes[:, c, :].bitcast(FP8X4),
                rhs_scale=wb_scales[:, c, :],
                start=True,
                stop=True,
            )
            live[("kv", c, j)] = kv

        def copy_out(c, j, copy):
            parts = live[("kv", c, j)][:].rearrange("p (h s d) -> p h s d", h=2, s=2)
            copy(live[("key", c)][:, :, j, 0:NOPE], parts[:, :, 0, :])
            copy(live[("value", c)][:, :, j, :], parts[:, :, 1, :])

        def store(c, j0, j1):
            heads = slice(2 * c, 2 * c + 2)
            for b in range(BATCH):
                nc.sync.dma_start(
                    out=key_view[b, :, heads, j0:j1, :],
                    in_=live[("key", c)][b:P:BATCH, :, j0:j1, :],
                )
                nc.sync.dma_start(
                    out=value_view[b, :, heads, j0:j1, :],
                    in_=live[("value", c)][b:P:BATCH, :, j0:j1, :],
                )

        keep_clock_up(WARM_START)
        for c in range(SPLIT_PAIRS):
            fill_rotated(c)
        arrivals = (
            ("wa", 0), ("wa", 1), ("wa", 2), ("wa", 3), ("x", 0), ("x", 1), ("x", 2), ("x", 3),
        )
        for n, (what, index) in enumerate(arrivals):
            transpose_pairs(what, index)
            keep_clock_up(1)
            if n == 1:
                spread_gain()
            regroup(what, index, 0, on_scalar)
            regroup(what, index, 1, on_vector if n % 2 == 0 else on_scalar)
            if n > 0:
                quantise(*arrivals[n - 1])
            if n == 1:
                order_gain()

        first_matmul(0)
        quantise("x", 3)
        first_matmul(1)
        root_mean_square(0)
        transpose_pairs("wb", 0)
        root_mean_square(1)
        normalise(0)
        transpose_pairs("wb", 1)
        regroup_rows(0, on_vector)
        transpose_normed(0)
        first_matmul(2)
        regroup_rows(1, on_scalar)
        normalise(1)
        quantise("wb", 0)
        regroup_normed(0, on_scalar)
        transpose_normed(1)
        transpose_pairs("wb", 2)
        root_mean_square(2)
        quantise("wb", 1)
        regroup_normed(1, on_vector)
        first_matmul(3)
        regroup_rows(2, on_scalar)
        quantise_normed(0)
        quantise_normed(1)
        normalise(2)
        second_matmul(0, 0)
        second_matmul(0, 1)
        root_mean_square(3)
        quantise("wb", 2)
        second_matmul(1, 0)
        second_matmul(1, 1)
        transpose_normed(2)
        copy_out(0, 0, on_vector)
        copy_out(0, 1, on_scalar)
        store(0, 0, 2)
        normalise(3)
        second_matmul(2, 0)
        second_matmul(2, 1)
        copy_out(1, 1, on_scalar)
        copy_out(1, 0, on_vector)
        store(1, 0, 2)
        regroup_normed(2, on_scalar)
        transpose_normed(3)
        transpose_pairs("wb", 3)
        quantise_normed(2)
        copy_out(2, 0, on_scalar)
        copy_out(2, 1, on_scalar)
        store(2, 0, 2)
        regroup_normed(3, on_vector)
        quantise_normed(3)
        for c in range(SPLIT_PAIRS):
            second_matmul(c, 2)
            second_matmul(c, 3)
        regroup_rows(3, on_vector)
        copy_out(0, 2, on_scalar)
        copy_out(0, 3, on_scalar)
        store(0, 2, 4)
        copy_out(1, 3, on_vector)
        copy_out(1, 2, on_scalar)
        store(1, 2, 4)
        quantise("wb", 3)
        copy_out(2, 3, on_scalar)
        copy_out(2, 2, on_vector)
        store(2, 2, 4)

        for c in range(SPLIT_PAIRS, PAIRS):
            if c + 1 < PAIRS:
                transpose_pairs("wb", c + 1)
                regroup_rows(c + 1, on_scalar)
            fill_rotated(c)
            for j in range(TILES):
                second_matmul(c, j)
            for j in range(TILES):
                copy_out(c, j, on_vector if j % 2 == 0 else on_scalar)
            store(c, 0, TILES)
            if c + 1 < PAIRS:
                quantise("wb", c + 1)
